import numpy as np
import ml_dtypes


def mxq(x, axis, fmt="e4m3"):
    dtype, down = {"e4m3": (ml_dtypes.float8_e4m3fn, 7), "e5m2": (ml_dtypes.float8_e5m2, 14)}[fmt]
    v = np.moveaxis(np.asarray(x, np.float32).astype(ml_dtypes.bfloat16).astype(np.float64), axis, -1)
    blocks = v.reshape(v.shape[:-1] + (-1, 32))
    amax = np.abs(blocks).max(-1, keepdims=True)
    byte = np.maximum(np.where(amax > 0, np.frexp(amax)[1] - 1 + 127, 0) - down, 1)
    scale = np.exp2(byte - 127.0)
    codes = (blocks / scale).astype(np.float32).astype(dtype).astype(np.float64)
    return np.moveaxis((codes * scale).reshape(v.shape), -1, axis)


WIDE = False


def mx_kscale(k):
    if not WIDE:
        return np.ones(k)
    levels = np.array([10, -10, 5, -5, 0])
    a = np.random.permutation(np.resize(levels, k // 512 * 4)).reshape(k // 512, 4)
    idx = np.arange(k)
    return np.exp2(a[idx // 512, idx % 128 // 32])


BF16 = ml_dtypes.bfloat16


def bf(x):
    return np.asarray(x, np.float32).astype(BF16)


def f64(x):
    return np.asarray(x).astype(np.float64)


N, D, NHID, C, P = 512, 512, 512, 128, 2
EPS = 1e-12
TAU = np.sqrt((P + 2.0) / (P * D))


def learn_graph(w, x):
    cf = w[:, None, :] * x[None, :, :]
    nrm = np.sqrt((cf * cf).sum(-1, keepdims=True))
    cf = cf / np.maximum(nrm, EPS)
    flat = cf.transpose(1, 0, 2).reshape(x.shape[0], -1)
    cq = mxq(flat, 1, "e4m3")
    att = (cq @ cq.T) / w.shape[0]
    att = np.where(att > 0, att, 0.0)
    return att / np.maximum(att.sum(-1, keepdims=True), EPS)


def setup_inputs():
    t = mx_kscale(NHID)
    a = np.maximum(np.random.standard_normal((N, N)), 0.0) * TAU + np.eye(N)
    wm = np.random.standard_normal((NHID, C))
    wm = wm - wm.mean(0, keepdims=True)
    return {"adj1": bf(a / a.sum(-1, keepdims=True)),
            "hw": bf(np.random.standard_normal((N, C)) * 4.0),
            "bg2": bf(np.random.standard_normal(C) * 0.04),
            "hm": bf(np.maximum(np.random.standard_normal((N, NHID)), 0.0) * t),
            "Wm2": bf(wm * 0.7 / np.sqrt(NHID) / t[:, None]),
            "bm2": bf(np.random.standard_normal(C) * 0.04),
            "w_gl2": bf(np.random.standard_normal((P, 2 * C)))}


def reference(adj1, hw, bg2, hm, Wm2, bm2, w_gl2):
    a1 = f64(adj1)
    z1 = (mxq(a1, 1, "e4m3") @ mxq(f64(hw), 0, "e4m3")) + f64(bg2)
    z2 = (mxq(f64(hm), 1, "e4m3") @ mxq(f64(Wm2), 0, "e4m3")) + f64(bm2)
    adj2 = learn_graph(f64(w_gl2), np.concatenate([z1, z2], axis=1))
    output = 0.5 * z1 + 0.5 * z2
    adj = 0.5 * a1 + 0.5 * adj2
    return output, adj

@@ -1,0 +1,256 @@
+from contextlib import ExitStack
+
+import concourse.mybir as mybir
+from concourse.masks import make_identity
+
+F32 = mybir.dt.float32
+BF16 = mybir.dt.bfloat16
+U32 = mybir.dt.uint32
+U8 = mybir.dt.uint8
+FP8X4 = mybir.dt.float8_e4m3fn_x4
+ACT = mybir.ActivationFunctionType
+ALU = mybir.AluOpType
+
+P = 128
+PACK = 4
+NODES = 512
+CHUNKS = NODES // P
+PAIRS = CHUNKS // 2
+FEAT = 128
+JOINED = 2 * FEAT
+PERSP = 2
+EPS = 1e-12
+
+FLOPS = 2 * NODES * NODES * FEAT * 2 + 2 * NODES * NODES * PERSP * JOINED
+
+
+def tile_pmodel_pb_s_kernel(tc, adj1, hw, bg2, hm, Wm2, bm2, w_gl2, out_0, out_1):
+    nc = tc.nc
+    with ExitStack() as ctx:
+        keep = ctx.enter_context(tc.tile_pool(name="keep", bufs=1))
+        psum = ctx.enter_context(tc.psum_pool(name="psum", bufs=1))
+        ctx.enter_context(tc.manual_schedule())
+
+        w_row = keep.tile([P, PERSP * JOINED], BF16)
+        bias_row = keep.tile([P, JOINED], BF16)
+        ones = keep.tile([P, P], BF16)
+        one = keep.tile([P, 1], F32)
+        nc.vector.memset(w_row[:], 0.0)
+        nc.vector.memset(ones[:], 1.0)
+        nc.vector.memset(one[:], 1.0)
+        nc.vector.memset(bias_row[:], 0.0)
+        nc.scalar.dma_start(out=w_row[0:1, :], in_=w_gl2.rearrange("(o p) f -> o (p f)", o=1))
+
+        table_warm = keep.tile([P, 1], F32)
+        nc.scalar.activation(out=table_warm[:], in_=one[:], func=ACT.Sqrt)
+
+        ident_f32 = keep.tile([P, P], F32)
+        ident_bf16 = keep.tile([P, P], BF16)
+        make_identity(nc, ident_f32[:])
+        make_identity(nc, ident_bf16[:])
+
+        adj_sb = keep.tile([P, CHUNKS, NODES], BF16)
+        hm_sb = keep.tile([P, CHUNKS, NODES], BF16)
+        for x_sb, x_dram in ((adj_sb, adj1), (hm_sb, hm)):
+            rows = x_dram.rearrange("(c p) k -> p c k", p=P)
+            for pair in range(PAIRS):
+                chunks = slice(2 * pair, 2 * pair + 2)
+                nc.sync.dma_start(out=x_sb[:, chunks, :], in_=rows[:, chunks, :])
+        weight_raw = keep.tile([P, 2, PACK, FEAT], BF16)
+        for m, weight in enumerate((hw, Wm2)):
+            nc.sync.dma_start(
+                out=weight_raw[:, m].rearrange("q (u e) f -> q u e f", u=2),
+                in_=weight.rearrange("(u q e) f -> q u e f", u=2, e=2),
+            )
+        nc.sync.dma_start(out=bias_row[0:1, 0:FEAT], in_=bg2.rearrange("(o f) -> o f", o=1))
+        nc.sync.dma_start(out=bias_row[0:1, FEAT:JOINED], in_=bm2.rearrange("(o f) -> o f", o=1))
+
+        w_spread = psum.tile([P, PERSP * JOINED], F32, tag="z0")
+        nc.tensor.matmul(out=w_spread[:], lhsT=ones[:], rhs=w_row[:], start=True, stop=True)
+        w_all = keep.tile([P, PERSP, JOINED], F32)
+        nc.scalar.copy(out=w_all[:].rearrange("n p f -> n (p f)"), in_=w_spread[:])
+
+        def make_operand(name):
+            return {
+                "grouped": keep.tile([P, CHUNKS, P, PACK], BF16, align_bytes=64, name=name + "_grouped"),
+                "codes": keep.tile([P, NODES], U32, align_bytes=64, name=name + "_codes"),
+                "scales": keep.tile([P, NODES], U8, align_bytes=64, name=name + "_scales"),
+            }
+
+        def flip_chunk(x_sb, operand, c):
+            words = x_sb[:].bitcast(F32)
+            flipped = psum.tile([P, 2, P], F32, tag="stage%d" % c, name="flipped")
+            for u in range(2):
+                nc.tensor.transpose(flipped[:, u, :], words[:, c, u * P : (u + 1) * P], ident_f32[:])
+            side_by_side = operand["grouped"][:].bitcast(F32)[:, c]
+            if c % 2 == 0:
+                nc.vector.tensor_copy(out=side_by_side, in_=flipped[:].rearrange("q u n -> q n u"))
+            else:
+                nc.scalar.copy(out=side_by_side, in_=flipped[:].rearrange("q u n -> q n u"))
+
+        def quantise_pair(operand, pair):
+            nodes = slice(2 * pair * P, (2 * pair + 2) * P)
+            nc.vector.quantize_mx(
+                out=operand["codes"][:, nodes].bitcast(FP8X4),
+                scales=operand["scales"][:, nodes],
+                in_=operand["grouped"][:, 2 * pair : 2 * pair + 2].rearrange("q c n t -> q (c n t)"),
+            )
+
+        adj_mx = make_operand("adj")
+        hm_mx = make_operand("hm")
+        waiting = None
+        for x_sb, operand in ((adj_sb, adj_mx), (hm_sb, hm_mx)):
+            for pair in range(PAIRS):
+                flip_chunk(x_sb, operand, 2 * pair)
+                flip_chunk(x_sb, operand, 2 * pair + 1)
+                if waiting is not None:
+                    quantise_pair(waiting[0], waiting[1])
+                waiting = (operand, pair)
+
+        bias_spread = psum.tile([P, JOINED], F32, tag="z3")
+        nc.tensor.matmul(out=bias_spread[:], lhsT=ones[:], rhs=bias_row[:], start=True, stop=True)
+        half_bias = keep.tile([P, JOINED], F32)
+        nc.scalar.activation(out=half_bias[:], in_=bias_spread[:], func=ACT.Copy, scale=0.5)
+
+        weight_grouped = keep.tile([P, 2, FEAT, PACK], BF16, align_bytes=64)
+        weight_codes = keep.tile([P, 2, FEAT], U32, align_bytes=64)
+        weight_scales = keep.tile([P, 2, FEAT], U8, align_bytes=64)
+        for m in range(2):
+            nc.vector.tensor_copy(out=weight_grouped[:, m], in_=weight_raw[:, m].rearrange("q t f -> q f t"))
+        for m in range(2):
+            nc.vector.quantize_mx(
+                out=weight_codes[:, m, :].bitcast(FP8X4),
+                scales=weight_scales[:, m, :],
+                in_=weight_grouped[:, m].rearrange("q f t -> q (f t)"),
+            )
+        quantise_pair(waiting[0], waiting[1])
+
+        z_banks = []
+        for c in range(CHUNKS):
+            nodes = slice(c * P, (c + 1) * P)
+            z = psum.tile([P, JOINED], F32, tag="z%d" % c, name="z")
+            for m, operand in enumerate((adj_mx, hm_mx)):
+                nc.tensor.matmul_mx(
+                    out=z[:, m * FEAT : (m + 1) * FEAT],
+                    lhsT=operand["codes"][:, nodes].bitcast(FP8X4),
+                    lhsT_scale=operand["scales"][:, nodes],
+                    rhs=weight_codes[:, m, :].bitcast(FP8X4),
+                    rhs_scale=weight_scales[:, m, :],
+                    start=True,
+                    stop=True,
+                )
+            z_banks.append(z)
+
+        half_x = keep.tile([P, CHUNKS, JOINED], F32)
+        weighted = keep.tile([P, CHUNKS, PERSP, JOINED], F32)
+        squares = keep.tile([P, JOINED], BF16)
+        norm_sq = keep.tile([P, CHUNKS, PERSP], F32)
+        norm = keep.tile([P, CHUNKS, PERSP], F32)
+        norm_floor = keep.tile([P, CHUNKS, PERSP], F32)
+        inv_norm = keep.tile([P, CHUNKS, PERSP], F32)
+        cf = keep.tile([P, CHUNKS, PERSP * JOINED], BF16)
+        cf_grouped = keep.tile([P, CHUNKS, P, PACK], BF16, align_bytes=64)
+        cf_codes = keep.tile([P, NODES], U32, align_bytes=64)
+        cf_scales = keep.tile([P, NODES], U8, align_bytes=64)
+        cf_banks = {}
+
+        def weigh(c):
+            nc.vector.scalar_tensor_tensor(
+                out=half_x[:, c, :], in0=z_banks[c][:], scalar=0.5, in1=half_bias[:], op0=ALU.mult, op1=ALU.add
+            )
+            nc.vector.tensor_tensor(
+                out=weighted[:, c],
+                in0=half_x[:, c, :].unsqueeze(1).to_broadcast([P, PERSP, JOINED]),
+                in1=w_all[:],
+                op=ALU.mult,
+            )
+            for p in range(PERSP):
+                nc.scalar.activation(
+                    out=squares[:], in_=weighted[:, c, p, :], func=ACT.Square, accum_out=norm_sq[:, c, p : p + 1]
+                )
+            nc.scalar.activation(out=norm[:, c, :], in_=norm_sq[:, c, :], func=ACT.Sqrt)
+
+        def normalise_and_flip(c):
+            nc.vector.tensor_scalar_max(out=norm_floor[:, c, :], in0=norm[:, c, :], scalar1=0.5 * EPS)
+            nc.vector.reciprocal(out=inv_norm[:, c, :], in_=norm_floor[:, c, :])
+            for p in range(PERSP):
+                nc.vector.tensor_scalar_mul(
+                    out=cf[:, c, p * JOINED : (p + 1) * JOINED],
+                    in0=weighted[:, c, p, :],
+                    scalar1=inv_norm[:, c, p : p + 1],
+                )
+            flipped = psum.tile([P, PACK, P], BF16, tag="stage%d" % c, name="cf_flipped")
+            for t in range(PACK):
+                nc.tensor.transpose(flipped[:, t, :], cf[:, c, t * P : (t + 1) * P], ident_bf16[:])
+            cf_banks[c] = flipped
+
+        def group_cf(c):
+            nc.scalar.copy(out=cf_grouped[:, c], in_=cf_banks[c][:].rearrange("q t n -> q n t"))
+
+        def quantise_cf(c):
+            nodes = slice(c * P, (c + 1) * P)
+            nc.vector.quantize_mx(
+                out=cf_codes[:, nodes].bitcast(FP8X4),
+                scales=cf_scales[:, nodes],
+                in_=cf_grouped[:, c].rearrange("q n t -> q (n t)"),
+            )
+
+        for step in range(CHUNKS + 2):
+            if step >= 2:
+                group_cf(step - 2)
+            if step < CHUNKS:
+                weigh(step)
+            if 1 <= step <= CHUNKS:
+                normalise_and_flip(step - 1)
+            if step >= 2:
+                quantise_cf(step - 2)
+
+        att_banks = []
+        for c in range(CHUNKS):
+            nodes = slice(c * P, (c + 1) * P)
+            att = psum.tile([P, NODES], F32, tag="stage%d" % c, name="att")
+            nc.tensor.matmul_mx(
+                out=att[:],
+                lhsT=cf_codes[:, nodes].bitcast(FP8X4),
+                lhsT_scale=cf_scales[:, nodes],
+                rhs=cf_codes[:].bitcast(FP8X4),
+                rhs_scale=cf_scales[:],
+                start=True,
+                stop=True,
+            )
+            att_banks.append(att)
+
+        output = keep.tile([P, CHUNKS, FEAT], F32)
+        nc.vector.tensor_tensor(out=output[:], in0=half_x[:, :, 0:FEAT], in1=half_x[:, :, FEAT:JOINED], op=ALU.add)
+        nc.sync.dma_start(out=out_0.rearrange("(c p) f -> p c f", p=P), in_=output[:])
+        half_adj = keep.tile([P, CHUNKS, NODES], BF16)
+        nc.vector.tensor_scalar_mul(out=half_adj[:], in0=adj_sb[:], scalar1=0.5)
+
+        masked = keep.tile([P, CHUNKS, NODES], F32)
+        row_sum = keep.tile([P, CHUNKS], F32)
+        twice_sum = keep.tile([P, CHUNKS], F32)
+        half_inv_sum = keep.tile([P, CHUNKS], F32)
+        adj = keep.tile([P, CHUNKS, NODES], F32)
+        adj_rows = out_1.rearrange("(c p) m -> p c m", p=P)
+        for c in range(CHUNKS):
+            nc.scalar.activation(
+                out=masked[:, c, :], in_=att_banks[c][:], func=ACT.Relu, scale=0.5, accum_out=row_sum[:, c : c + 1]
+            )
+            nc.vector.tensor_scalar(
+                out=twice_sum[:, c : c + 1],
+                in0=row_sum[:, c : c + 1],
+                scalar1=EPS,
+                scalar2=2.0,
+                op0=ALU.max,
+                op1=ALU.mult,
+            )
+            nc.vector.reciprocal(out=half_inv_sum[:, c : c + 1], in_=twice_sum[:, c : c + 1])
+            nc.vector.scalar_tensor_tensor(
+                out=adj[:, c, :],
+                in0=masked[:, c, :],
+                scalar=half_inv_sum[:, c : c + 1],
+                in1=half_adj[:, c, :],
+                op0=ALU.mult,
+                op1=ALU.add,
+            )
+            nc.sync.dma_start(out=adj_rows[:, c, :], in_=adj[:, c, :])

@@ -49,26 +49,24 @@ def tile_pmodel_pb_s_kernel(tc, adj1, hw, bg2, hm, Wm2, bm2, w_gl2, out_0, out_1
         make_identity(nc, ident_f32[:])
         make_identity(nc, ident_bf16[:])
 
-        adj_sb = keep.tile([P, CHUNKS, NODES], BF16)
-        hm_sb = keep.tile([P, CHUNKS, NODES], BF16)
-        for x_sb, x_dram in ((adj_sb, adj1), (hm_sb, hm)):
+        def load_nodes(x_sb, x_dram):
             rows = x_dram.rearrange("(c p) k -> p c k", p=P)
             for pair in range(PAIRS):
                 chunks = slice(2 * pair, 2 * pair + 2)
                 nc.sync.dma_start(out=x_sb[:, chunks, :], in_=rows[:, chunks, :])
+
+        adj_sb = keep.tile([P, CHUNKS, NODES], BF16)
+        hm_sb = keep.tile([P, CHUNKS, NODES], BF16)
         weight_raw = keep.tile([P, 2, PACK, FEAT], BF16)
+        load_nodes(adj_sb, adj1)
         for m, weight in enumerate((hw, Wm2)):
             nc.sync.dma_start(
                 out=weight_raw[:, m].rearrange("q (u e) f -> q u e f", u=2),
                 in_=weight.rearrange("(u q e) f -> q u e f", u=2, e=2),
             )
+        load_nodes(hm_sb, hm)
         nc.sync.dma_start(out=bias_row[0:1, 0:FEAT], in_=bg2.rearrange("(o f) -> o f", o=1))
         nc.sync.dma_start(out=bias_row[0:1, FEAT:JOINED], in_=bm2.rearrange("(o f) -> o f", o=1))
-
-        w_spread = psum.tile([P, PERSP * JOINED], F32, tag="z0")
-        nc.tensor.matmul(out=w_spread[:], lhsT=ones[:], rhs=w_row[:], start=True, stop=True)
-        w_all = keep.tile([P, PERSP, JOINED], F32)
-        nc.scalar.copy(out=w_all[:].rearrange("n p f -> n (p f)"), in_=w_spread[:])
 
         def make_operand(name):
             return {
@@ -77,16 +75,12 @@ def tile_pmodel_pb_s_kernel(tc, adj1, hw, bg2, hm, Wm2, bm2, w_gl2, out_0, out_1
                 "scales": keep.tile([P, NODES], U8, align_bytes=64, name=name + "_scales"),
             }
 
-        def flip_chunk(x_sb, operand, c):
+        def flip_chunk(x_sb, operand, c, copy):
             words = x_sb[:].bitcast(F32)
             flipped = psum.tile([P, 2, P], F32, tag="stage%d" % c, name="flipped")
             for u in range(2):
                 nc.tensor.transpose(flipped[:, u, :], words[:, c, u * P : (u + 1) * P], ident_f32[:])
-            side_by_side = operand["grouped"][:].bitcast(F32)[:, c]
-            if c % 2 == 0:
-                nc.vector.tensor_copy(out=side_by_side, in_=flipped[:].rearrange("q u n -> q n u"))
-            else:
-                nc.scalar.copy(out=side_by_side, in_=flipped[:].rearrange("q u n -> q n u"))
+            copy(out=operand["grouped"][:].bitcast(F32)[:, c], in_=flipped[:].rearrange("q u n -> q n u"))
 
         def quantise_pair(operand, pair):
             nodes = slice(2 * pair * P, (2 * pair + 2) * P)
@@ -97,33 +91,36 @@ def tile_pmodel_pb_s_kernel(tc, adj1, hw, bg2, hm, Wm2, bm2, w_gl2, out_0, out_1
             )
 
         adj_mx = make_operand("adj")
+        for c in range(CHUNKS):
+            flip_chunk(adj_sb, adj_mx, c, nc.vector.tensor_copy)
+        for pair in range(PAIRS):
+            quantise_pair(adj_mx, pair)
+
+        w_spread = psum.tile([P, PERSP * JOINED], F32, tag="z0")
+        nc.tensor.matmul(out=w_spread[:], lhsT=ones[:], rhs=w_row[:], start=True, stop=True)
+        w_all = keep.tile([P, PERSP, JOINED], F32)
+        nc.scalar.copy(out=w_all[:].rearrange("n p f -> n (p f)"), in_=w_spread[:])
+
+        weight_grouped = keep.tile([P, 2, FEAT, PACK], BF16, align_bytes=64)
+        weight_codes = keep.tile([P, 2, FEAT], U32, align_bytes=64)
+        weight_scales = keep.tile([P, 2, FEAT], U8, align_bytes=64)
+        nc.vector.tensor_copy(out=weight_grouped[:], in_=weight_raw[:].rearrange("q m t f -> q m f t"))
+        nc.vector.quantize_mx(
+            out=weight_codes[:].rearrange("q m f -> q (m f)").bitcast(FP8X4),
+            scales=weight_scales[:].rearrange("q m f -> q (m f)"),
+            in_=weight_grouped[:].rearrange("q m f t -> q (m f t)"),
+        )
+
         hm_mx = make_operand("hm")
-        waiting = None
-        for x_sb, operand in ((adj_sb, adj_mx), (hm_sb, hm_mx)):
-            for pair in range(PAIRS):
-                flip_chunk(x_sb, operand, 2 * pair)
-                flip_chunk(x_sb, operand, 2 * pair + 1)
-                if waiting is not None:
-                    quantise_pair(waiting[0], waiting[1])
-                waiting = (operand, pair)
+        for pair in range(PAIRS):
+            flip_chunk(hm_sb, hm_mx, 2 * pair, nc.scalar.copy)
+            flip_chunk(hm_sb, hm_mx, 2 * pair + 1, nc.scalar.copy)
+            quantise_pair(hm_mx, pair)
 
         bias_spread = psum.tile([P, JOINED], F32, tag="z3")
         nc.tensor.matmul(out=bias_spread[:], lhsT=ones[:], rhs=bias_row[:], start=True, stop=True)
         half_bias = keep.tile([P, JOINED], F32)
         nc.scalar.activation(out=half_bias[:], in_=bias_spread[:], func=ACT.Copy, scale=0.5)
-
-        weight_grouped = keep.tile([P, 2, FEAT, PACK], BF16, align_bytes=64)
-        weight_codes = keep.tile([P, 2, FEAT], U32, align_bytes=64)
-        weight_scales = keep.tile([P, 2, FEAT], U8, align_bytes=64)
-        for m in range(2):
-            nc.vector.tensor_copy(out=weight_grouped[:, m], in_=weight_raw[:, m].rearrange("q t f -> q f t"))
-        for m in range(2):
-            nc.vector.quantize_mx(
-                out=weight_codes[:, m, :].bitcast(FP8X4),
-                scales=weight_scales[:, m, :],
-                in_=weight_grouped[:, m].rearrange("q f t -> q (f t)"),
-            )
-        quantise_pair(waiting[0], waiting[1])
 
         z_banks = []
         for c in range(CHUNKS):
@@ -141,6 +138,9 @@ def tile_pmodel_pb_s_kernel(tc, adj1, hw, bg2, hm, Wm2, bm2, w_gl2, out_0, out_1
                 )
             z_banks.append(z)
 
+        half_adj = keep.tile([P, CHUNKS, NODES], BF16)
+        nc.scalar.mul(out=half_adj[:, 0:2, :], in_=adj_sb[:, 0:2, :], mul=0.5)
+
         half_x = keep.tile([P, CHUNKS, JOINED], F32)
         weighted = keep.tile([P, CHUNKS, PERSP, JOINED], F32)
         squares = keep.tile([P, JOINED], BF16)
@@ -152,58 +152,58 @@ def tile_pmodel_pb_s_kernel(tc, adj1, hw, bg2, hm, Wm2, bm2, w_gl2, out_0, out_1
         cf_grouped = keep.tile([P, CHUNKS, P, PACK], BF16, align_bytes=64)
         cf_codes = keep.tile([P, NODES], U32, align_bytes=64)
         cf_scales = keep.tile([P, NODES], U8, align_bytes=64)
-        cf_banks = {}
 
-        def weigh(c):
-            nc.vector.scalar_tensor_tensor(
-                out=half_x[:, c, :], in0=z_banks[c][:], scalar=0.5, in1=half_bias[:], op0=ALU.mult, op1=ALU.add
-            )
-            nc.vector.tensor_tensor(
-                out=weighted[:, c],
-                in0=half_x[:, c, :].unsqueeze(1).to_broadcast([P, PERSP, JOINED]),
-                in1=w_all[:],
-                op=ALU.mult,
-            )
-            for p in range(PERSP):
-                nc.scalar.activation(
-                    out=squares[:], in_=weighted[:, c, p, :], func=ACT.Square, accum_out=norm_sq[:, c, p : p + 1]
+        for pair in range(PAIRS):
+            chunks = slice(2 * pair, 2 * pair + 2)
+            for c in (2 * pair, 2 * pair + 1):
+                nc.vector.scalar_tensor_tensor(
+                    out=half_x[:, c, :], in0=z_banks[c][:], scalar=0.5, in1=half_bias[:], op0=ALU.mult, op1=ALU.add
                 )
-            nc.scalar.activation(out=norm[:, c, :], in_=norm_sq[:, c, :], func=ACT.Sqrt)
-
-        def normalise_and_flip(c):
-            nc.vector.tensor_scalar_max(out=norm_floor[:, c, :], in0=norm[:, c, :], scalar1=0.5 * EPS)
-            nc.vector.reciprocal(out=inv_norm[:, c, :], in_=norm_floor[:, c, :])
-            for p in range(PERSP):
-                nc.vector.tensor_scalar_mul(
-                    out=cf[:, c, p * JOINED : (p + 1) * JOINED],
-                    in0=weighted[:, c, p, :],
-                    scalar1=inv_norm[:, c, p : p + 1],
+                nc.vector.tensor_tensor(
+                    out=weighted[:, c],
+                    in0=half_x[:, c, :].unsqueeze(1).to_broadcast([P, PERSP, JOINED]),
+                    in1=w_all[:],
+                    op=ALU.mult,
                 )
-            flipped = psum.tile([P, PACK, P], BF16, tag="stage%d" % c, name="cf_flipped")
-            for t in range(PACK):
-                nc.tensor.transpose(flipped[:, t, :], cf[:, c, t * P : (t + 1) * P], ident_bf16[:])
-            cf_banks[c] = flipped
+                for p in range(PERSP):
+                    nc.scalar.activation(
+                        out=squares[:], in_=weighted[:, c, p, :], func=ACT.Square, accum_out=norm_sq[:, c, p : p + 1]
+                    )
+            nc.scalar.activation(out=norm[:, chunks, :], in_=norm_sq[:, chunks, :], func=ACT.Sqrt)
 
-        def group_cf(c):
-            nc.scalar.copy(out=cf_grouped[:, c], in_=cf_banks[c][:].rearrange("q t n -> q n t"))
+        cf_banks = []
+        for pair in range(PAIRS):
+            chunks = slice(2 * pair, 2 * pair + 2)
+            nc.vector.tensor_scalar_max(out=norm_floor[:, chunks, :], in0=norm[:, chunks, :], scalar1=0.5 * EPS)
+            nc.vector.reciprocal(out=inv_norm[:, chunks, :], in_=norm_floor[:, chunks, :])
+            for c in (2 * pair, 2 * pair + 1):
+                for p in range(PERSP):
+                    nc.vector.tensor_scalar_mul(
+                        out=cf[:, c, p * JOINED : (p + 1) * JOINED],
+                        in0=weighted[:, c, p, :],
+                        scalar1=inv_norm[:, c, p : p + 1],
+                    )
+                cf_flipped = psum.tile([P, PACK, P], BF16, tag="stage%d" % c, name="cf_flipped")
+                for t in range(PACK):
+                    nc.tensor.transpose(cf_flipped[:, t, :], cf[:, c, t * P : (t + 1) * P], ident_bf16[:])
+                cf_banks.append(cf_flipped)
 
-        def quantise_cf(c):
+        def group_and_quantise(c):
             nodes = slice(c * P, (c + 1) * P)
+            nc.scalar.copy(out=cf_grouped[:, c], in_=cf_banks[c][:].rearrange("q t n -> q n t"))
             nc.vector.quantize_mx(
                 out=cf_codes[:, nodes].bitcast(FP8X4),
                 scales=cf_scales[:, nodes],
                 in_=cf_grouped[:, c].rearrange("q n t -> q (n t)"),
             )
 
-        for step in range(CHUNKS + 2):
-            if step >= 2:
-                group_cf(step - 2)
-            if step < CHUNKS:
-                weigh(step)
-            if 1 <= step <= CHUNKS:
-                normalise_and_flip(step - 1)
-            if step >= 2:
-                quantise_cf(step - 2)
+        group_and_quantise(0)
+        group_and_quantise(1)
+        output = keep.tile([P, CHUNKS, FEAT], F32)
+        nc.vector.tensor_tensor(out=output[:], in0=half_x[:, :, 0:FEAT], in1=half_x[:, :, FEAT:JOINED], op=ALU.add)
+        nc.sync.dma_start(out=out_0.rearrange("(c p) f -> p c f", p=P), in_=output[:])
+        group_and_quantise(2)
+        group_and_quantise(3)
 
         att_banks = []
         for c in range(CHUNKS):
@@ -220,11 +220,7 @@ def tile_pmodel_pb_s_kernel(tc, adj1, hw, bg2, hm, Wm2, bm2, w_gl2, out_0, out_1
             )
             att_banks.append(att)
 
-        output = keep.tile([P, CHUNKS, FEAT], F32)
-        nc.vector.tensor_tensor(out=output[:], in0=half_x[:, :, 0:FEAT], in1=half_x[:, :, FEAT:JOINED], op=ALU.add)
-        nc.sync.dma_start(out=out_0.rearrange("(c p) f -> p c f", p=P), in_=output[:])
-        half_adj = keep.tile([P, CHUNKS, NODES], BF16)
-        nc.vector.tensor_scalar_mul(out=half_adj[:], in0=adj_sb[:], scalar1=0.5)
+        nc.vector.tensor_scalar_mul(out=half_adj[:, 2:4, :], in0=adj_sb[:, 2:4, :], scalar1=0.5)
 
         masked = keep.tile([P, CHUNKS, NODES], F32)
         row_sum = keep.tile([P, CHUNKS], F32)

@@ -35,11 +35,12 @@ def tile_pmodel_pb_s_kernel(tc, adj1, hw, bg2, hm, Wm2, bm2, w_gl2, out_0, out_1
         bias_row = keep.tile([P, JOINED], BF16)
         ones = keep.tile([P, P], BF16)
         one = keep.tile([P, 1], F32)
-        nc.vector.memset(w_row[:], 0.0)
+        nc.vector.memset(bias_row[:], 0.0)
         nc.vector.memset(ones[:], 1.0)
         nc.vector.memset(one[:], 1.0)
-        nc.vector.memset(bias_row[:], 0.0)
-        nc.scalar.dma_start(out=w_row[0:1, :], in_=w_gl2.rearrange("(o p) f -> o (p f)", o=1))
+        nc.vector.memset(w_row[:], 0.0)
+        nc.scalar.dma_start(out=bias_row[0:1, 0:FEAT], in_=bg2.rearrange("(o f) -> o f", o=1))
+        nc.scalar.dma_start(out=bias_row[0:1, FEAT:JOINED], in_=bm2.rearrange("(o f) -> o f", o=1))
 
         table_warm = keep.tile([P, 1], F32)
         nc.scalar.activation(out=table_warm[:], in_=one[:], func=ACT.Sqrt)
@@ -50,7 +51,7 @@ def tile_pmodel_pb_s_kernel(tc, adj1, hw, bg2, hm, Wm2, bm2, w_gl2, out_0, out_1
         make_identity(nc, ident_bf16[:])
 
         def load_nodes(x_sb, x_dram):
-            rows = x_dram.rearrange("(c p) k -> p c k", p=P)
+            rows = x_dram.rearrange("(p c) k -> p c k", c=CHUNKS)
             for pair in range(PAIRS):
                 chunks = slice(2 * pair, 2 * pair + 2)
                 nc.sync.dma_start(out=x_sb[:, chunks, :], in_=rows[:, chunks, :])
@@ -65,8 +66,7 @@ def tile_pmodel_pb_s_kernel(tc, adj1, hw, bg2, hm, Wm2, bm2, w_gl2, out_0, out_1
                 in_=weight.rearrange("(u q e) f -> q u e f", u=2, e=2),
             )
         load_nodes(hm_sb, hm)
-        nc.sync.dma_start(out=bias_row[0:1, 0:FEAT], in_=bg2.rearrange("(o f) -> o f", o=1))
-        nc.sync.dma_start(out=bias_row[0:1, FEAT:JOINED], in_=bm2.rearrange("(o f) -> o f", o=1))
+        nc.sync.dma_start(out=w_row[0:1, :], in_=w_gl2.rearrange("(o p) f -> o (p f)", o=1))
 
         def make_operand(name):
             return {
@@ -96,10 +96,13 @@ def tile_pmodel_pb_s_kernel(tc, adj1, hw, bg2, hm, Wm2, bm2, w_gl2, out_0, out_1
         for pair in range(PAIRS):
             quantise_pair(adj_mx, pair)
 
-        w_spread = psum.tile([P, PERSP * JOINED], F32, tag="z0")
-        nc.tensor.matmul(out=w_spread[:], lhsT=ones[:], rhs=w_row[:], start=True, stop=True)
-        w_all = keep.tile([P, PERSP, JOINED], F32)
-        nc.scalar.copy(out=w_all[:].rearrange("n p f -> n (p f)"), in_=w_spread[:])
+        bias_spread = psum.tile([P, JOINED], F32, tag="z3")
+        nc.tensor.matmul(out=bias_spread[:], lhsT=ones[:], rhs=bias_row[:], start=True, stop=True)
+        half_bias = keep.tile([P, JOINED], F32)
+        nc.scalar.activation(out=half_bias[:], in_=bias_spread[:], func=ACT.Copy, scale=0.5)
+
+        half_adj = keep.tile([P, CHUNKS, NODES], BF16)
+        nc.scalar.mul(out=half_adj[:, 0:2, :], in_=adj_sb[:, 0:2, :], mul=0.5)
 
         weight_grouped = keep.tile([P, 2, FEAT, PACK], BF16, align_bytes=64)
         weight_codes = keep.tile([P, 2, FEAT], U32, align_bytes=64)
@@ -117,13 +120,7 @@ def tile_pmodel_pb_s_kernel(tc, adj1, hw, bg2, hm, Wm2, bm2, w_gl2, out_0, out_1
             flip_chunk(hm_sb, hm_mx, 2 * pair + 1, nc.scalar.copy)
             quantise_pair(hm_mx, pair)
 
-        bias_spread = psum.tile([P, JOINED], F32, tag="z3")
-        nc.tensor.matmul(out=bias_spread[:], lhsT=ones[:], rhs=bias_row[:], start=True, stop=True)
-        half_bias = keep.tile([P, JOINED], F32)
-        nc.scalar.activation(out=half_bias[:], in_=bias_spread[:], func=ACT.Copy, scale=0.5)
-
-        z_banks = []
-        for c in range(CHUNKS):
+        def multiply(c):
             nodes = slice(c * P, (c + 1) * P)
             z = psum.tile([P, JOINED], F32, tag="z%d" % c, name="z")
             for m, operand in enumerate((adj_mx, hm_mx)):
@@ -136,10 +133,18 @@ def tile_pmodel_pb_s_kernel(tc, adj1, hw, bg2, hm, Wm2, bm2, w_gl2, out_0, out_1
                     start=True,
                     stop=True,
                 )
-            z_banks.append(z)
+            return z
 
-        half_adj = keep.tile([P, CHUNKS, NODES], BF16)
-        nc.scalar.mul(out=half_adj[:, 0:2, :], in_=adj_sb[:, 0:2, :], mul=0.5)
+        z_banks = [multiply(0), multiply(1)]
+
+        w_0 = psum.tile([P, JOINED], F32, tag="stage0")
+        w_spread_1 = psum.tile([P, JOINED], F32, tag="stage1")
+        nc.tensor.matmul(out=w_0[:], lhsT=ones[:], rhs=w_row[:, 0:JOINED], start=True, stop=True)
+        nc.tensor.matmul(out=w_spread_1[:], lhsT=ones[:], rhs=w_row[:, JOINED : 2 * JOINED], start=True, stop=True)
+        w_1 = keep.tile([P, JOINED], F32)
+        nc.scalar.copy(out=w_1[:], in_=w_spread_1[:])
+
+        z_banks.extend([multiply(2), multiply(3)])
 
         half_x = keep.tile([P, CHUNKS, JOINED], F32)
         weighted = keep.tile([P, CHUNKS, PERSP, JOINED], F32)
@@ -159,12 +164,8 @@ def tile_pmodel_pb_s_kernel(tc, adj1, hw, bg2, hm, Wm2, bm2, w_gl2, out_0, out_1
                 nc.vector.scalar_tensor_tensor(
                     out=half_x[:, c, :], in0=z_banks[c][:], scalar=0.5, in1=half_bias[:], op0=ALU.mult, op1=ALU.add
                 )
-                nc.vector.tensor_tensor(
-                    out=weighted[:, c],
-                    in0=half_x[:, c, :].unsqueeze(1).to_broadcast([P, PERSP, JOINED]),
-                    in1=w_all[:],
-                    op=ALU.mult,
-                )
+                nc.vector.tensor_tensor(out=weighted[:, c, 0, :], in0=half_x[:, c, :], in1=w_0[:], op=ALU.mult)
+                nc.gpsimd.tensor_tensor(out=weighted[:, c, 1, :], in0=half_x[:, c, :], in1=w_1[:], op=ALU.mult)
                 for p in range(PERSP):
                     nc.scalar.activation(
                         out=squares[:], in_=weighted[:, c, p, :], func=ACT.Square, accum_out=norm_sq[:, c, p : p + 1]
@@ -172,7 +173,8 @@ def tile_pmodel_pb_s_kernel(tc, adj1, hw, bg2, hm, Wm2, bm2, w_gl2, out_0, out_1
             nc.scalar.activation(out=norm[:, chunks, :], in_=norm_sq[:, chunks, :], func=ACT.Sqrt)
 
         cf_banks = []
-        for pair in range(PAIRS):
+
+        def normalise_and_flip(pair):
             chunks = slice(2 * pair, 2 * pair + 2)
             nc.vector.tensor_scalar_max(out=norm_floor[:, chunks, :], in0=norm[:, chunks, :], scalar1=0.5 * EPS)
             nc.vector.reciprocal(out=inv_norm[:, chunks, :], in_=norm_floor[:, chunks, :])
@@ -188,22 +190,22 @@ def tile_pmodel_pb_s_kernel(tc, adj1, hw, bg2, hm, Wm2, bm2, w_gl2, out_0, out_1
                     nc.tensor.transpose(cf_flipped[:, t, :], cf[:, c, t * P : (t + 1) * P], ident_bf16[:])
                 cf_banks.append(cf_flipped)
 
-        def group_and_quantise(c):
+        normalise_and_flip(0)
+        output = keep.tile([P, CHUNKS, FEAT], F32)
+        nc.vector.tensor_tensor(out=output[:], in0=half_x[:, :, 0:FEAT], in1=half_x[:, :, FEAT:JOINED], op=ALU.add)
+        nc.sync.dma_start(out=out_0.rearrange("(p c) f -> p c f", c=CHUNKS), in_=output[:])
+        normalise_and_flip(1)
+
+        for c in range(CHUNKS):
+            copy = nc.vector.tensor_copy if c == CHUNKS - 2 else nc.scalar.copy
+            copy(out=cf_grouped[:, c], in_=cf_banks[c][:].rearrange("q t n -> q n t"))
+        for c in range(CHUNKS):
             nodes = slice(c * P, (c + 1) * P)
-            nc.scalar.copy(out=cf_grouped[:, c], in_=cf_banks[c][:].rearrange("q t n -> q n t"))
             nc.vector.quantize_mx(
                 out=cf_codes[:, nodes].bitcast(FP8X4),
                 scales=cf_scales[:, nodes],
                 in_=cf_grouped[:, c].rearrange("q n t -> q (n t)"),
             )
-
-        group_and_quantise(0)
-        group_and_quantise(1)
-        output = keep.tile([P, CHUNKS, FEAT], F32)
-        nc.vector.tensor_tensor(out=output[:], in0=half_x[:, :, 0:FEAT], in1=half_x[:, :, FEAT:JOINED], op=ALU.add)
-        nc.sync.dma_start(out=out_0.rearrange("(c p) f -> p c f", p=P), in_=output[:])
-        group_and_quantise(2)
-        group_and_quantise(3)
 
         att_banks = []
         for c in range(CHUNKS):
@@ -227,10 +229,14 @@ def tile_pmodel_pb_s_kernel(tc, adj1, hw, bg2, hm, Wm2, bm2, w_gl2, out_0, out_1
         twice_sum = keep.tile([P, CHUNKS], F32)
         half_inv_sum = keep.tile([P, CHUNKS], F32)
         adj = keep.tile([P, CHUNKS, NODES], F32)
-        adj_rows = out_1.rearrange("(c p) m -> p c m", p=P)
+        adj_rows = out_1.rearrange("(p c) m -> p c m", c=CHUNKS)
         for c in range(CHUNKS):
             nc.scalar.activation(
-                out=masked[:, c, :], in_=att_banks[c][:], func=ACT.Relu, scale=0.5, accum_out=row_sum[:, c : c + 1]
+                out=masked[:, c, :].rearrange("n (j c) -> n j c", c=CHUNKS),
+                in_=att_banks[c][:].rearrange("n (c j) -> n j c", c=CHUNKS),
+                func=ACT.Relu,
+                scale=0.5,
+                accum_out=row_sum[:, c : c + 1],
             )
             nc.vector.tensor_scalar(
                 out=twice_sum[:, c : c + 1],

@@ -35,12 +35,11 @@ def tile_pmodel_pb_s_kernel(tc, adj1, hw, bg2, hm, Wm2, bm2, w_gl2, out_0, out_1
         bias_row = keep.tile([P, JOINED], BF16)
         ones = keep.tile([P, P], BF16)
         one = keep.tile([P, 1], F32)
-        nc.vector.memset(bias_row[:], 0.0)
+        nc.vector.memset(w_row[:], 0.0)
         nc.vector.memset(ones[:], 1.0)
         nc.vector.memset(one[:], 1.0)
-        nc.vector.memset(w_row[:], 0.0)
-        nc.scalar.dma_start(out=bias_row[0:1, 0:FEAT], in_=bg2.rearrange("(o f) -> o f", o=1))
-        nc.scalar.dma_start(out=bias_row[0:1, FEAT:JOINED], in_=bm2.rearrange("(o f) -> o f", o=1))
+        nc.vector.memset(bias_row[:], 0.0)
+        nc.scalar.dma_start(out=w_row[0:1, :], in_=w_gl2.rearrange("(o p) f -> o (p f)", o=1))
 
         table_warm = keep.tile([P, 1], F32)
         nc.scalar.activation(out=table_warm[:], in_=one[:], func=ACT.Sqrt)
@@ -51,7 +50,7 @@ def tile_pmodel_pb_s_kernel(tc, adj1, hw, bg2, hm, Wm2, bm2, w_gl2, out_0, out_1
         make_identity(nc, ident_bf16[:])
 
         def load_nodes(x_sb, x_dram):
-            rows = x_dram.rearrange("(p c) k -> p c k", c=CHUNKS)
+            rows = x_dram.rearrange("(c p) k -> p c k", p=P)
             for pair in range(PAIRS):
                 chunks = slice(2 * pair, 2 * pair + 2)
                 nc.sync.dma_start(out=x_sb[:, chunks, :], in_=rows[:, chunks, :])
@@ -66,7 +65,8 @@ def tile_pmodel_pb_s_kernel(tc, adj1, hw, bg2, hm, Wm2, bm2, w_gl2, out_0, out_1
                 in_=weight.rearrange("(u q e) f -> q u e f", u=2, e=2),
             )
         load_nodes(hm_sb, hm)
-        nc.sync.dma_start(out=w_row[0:1, :], in_=w_gl2.rearrange("(o p) f -> o (p f)", o=1))
+        nc.sync.dma_start(out=bias_row[0:1, 0:FEAT], in_=bg2.rearrange("(o f) -> o f", o=1))
+        nc.sync.dma_start(out=bias_row[0:1, FEAT:JOINED], in_=bm2.rearrange("(o f) -> o f", o=1))
 
         def make_operand(name):
             return {
@@ -93,21 +93,18 @@ def tile_pmodel_pb_s_kernel(tc, adj1, hw, bg2, hm, Wm2, bm2, w_gl2, out_0, out_1
         adj_mx = make_operand("adj")
         for c in range(CHUNKS):
             flip_chunk(adj_sb, adj_mx, c, nc.vector.tensor_copy)
-        for pair in range(PAIRS):
-            quantise_pair(adj_mx, pair)
 
-        bias_spread = psum.tile([P, JOINED], F32, tag="z3")
-        nc.tensor.matmul(out=bias_spread[:], lhsT=ones[:], rhs=bias_row[:], start=True, stop=True)
-        half_bias = keep.tile([P, JOINED], F32)
-        nc.scalar.activation(out=half_bias[:], in_=bias_spread[:], func=ACT.Copy, scale=0.5)
-
-        half_adj = keep.tile([P, CHUNKS, NODES], BF16)
-        nc.scalar.mul(out=half_adj[:, 0:2, :], in_=adj_sb[:, 0:2, :], mul=0.5)
+        w_spread = psum.tile([P, PERSP * JOINED], F32, tag="z0")
+        nc.tensor.matmul(out=w_spread[:], lhsT=ones[:], rhs=w_row[:], start=True, stop=True)
+        w_all = keep.tile([P, PERSP, JOINED], F32)
+        nc.scalar.copy(out=w_all[:].rearrange("n p f -> n (p f)"), in_=w_spread[:])
 
         weight_grouped = keep.tile([P, 2, FEAT, PACK], BF16, align_bytes=64)
         weight_codes = keep.tile([P, 2, FEAT], U32, align_bytes=64)
         weight_scales = keep.tile([P, 2, FEAT], U8, align_bytes=64)
         nc.vector.tensor_copy(out=weight_grouped[:], in_=weight_raw[:].rearrange("q m t f -> q m f t"))
+        for pair in range(PAIRS):
+            quantise_pair(adj_mx, pair)
         nc.vector.quantize_mx(
             out=weight_codes[:].rearrange("q m f -> q (m f)").bitcast(FP8X4),
             scales=weight_scales[:].rearrange("q m f -> q (m f)"),
@@ -120,7 +117,13 @@ def tile_pmodel_pb_s_kernel(tc, adj1, hw, bg2, hm, Wm2, bm2, w_gl2, out_0, out_1
             flip_chunk(hm_sb, hm_mx, 2 * pair + 1, nc.scalar.copy)
             quantise_pair(hm_mx, pair)
 
-        def multiply(c):
+        bias_spread = psum.tile([P, JOINED], F32, tag="z3")
+        nc.tensor.matmul(out=bias_spread[:], lhsT=ones[:], rhs=bias_row[:], start=True, stop=True)
+        half_bias = keep.tile([P, JOINED], F32)
+        nc.scalar.activation(out=half_bias[:], in_=bias_spread[:], func=ACT.Copy, scale=0.5)
+
+        z_banks = []
+        for c in range(CHUNKS):
             nodes = slice(c * P, (c + 1) * P)
             z = psum.tile([P, JOINED], F32, tag="z%d" % c, name="z")
             for m, operand in enumerate((adj_mx, hm_mx)):
@@ -133,18 +136,10 @@ def tile_pmodel_pb_s_kernel(tc, adj1, hw, bg2, hm, Wm2, bm2, w_gl2, out_0, out_1
                     start=True,
                     stop=True,
                 )
-            return z
+            z_banks.append(z)
 
-        z_banks = [multiply(0), multiply(1)]
-
-        w_0 = psum.tile([P, JOINED], F32, tag="stage0")
-        w_spread_1 = psum.tile([P, JOINED], F32, tag="stage1")
-        nc.tensor.matmul(out=w_0[:], lhsT=ones[:], rhs=w_row[:, 0:JOINED], start=True, stop=True)
-        nc.tensor.matmul(out=w_spread_1[:], lhsT=ones[:], rhs=w_row[:, JOINED : 2 * JOINED], start=True, stop=True)
-        w_1 = keep.tile([P, JOINED], F32)
-        nc.scalar.copy(out=w_1[:], in_=w_spread_1[:])
-
-        z_banks.extend([multiply(2), multiply(3)])
+        half_adj = keep.tile([P, CHUNKS, NODES], BF16)
+        nc.scalar.mul(out=half_adj[:, 0:2, :], in_=adj_sb[:, 0:2, :], mul=0.5)
 
         half_x = keep.tile([P, CHUNKS, JOINED], F32)
         weighted = keep.tile([P, CHUNKS, PERSP, JOINED], F32)
@@ -158,43 +153,55 @@ def tile_pmodel_pb_s_kernel(tc, adj1, hw, bg2, hm, Wm2, bm2, w_gl2, out_0, out_1
         cf_codes = keep.tile([P, NODES], U32, align_bytes=64)
         cf_scales = keep.tile([P, NODES], U8, align_bytes=64)
 
-        for pair in range(PAIRS):
-            chunks = slice(2 * pair, 2 * pair + 2)
-            for c in (2 * pair, 2 * pair + 1):
-                nc.vector.scalar_tensor_tensor(
-                    out=half_x[:, c, :], in0=z_banks[c][:], scalar=0.5, in1=half_bias[:], op0=ALU.mult, op1=ALU.add
+        def add_bias(c):
+            nc.vector.scalar_tensor_tensor(
+                out=half_x[:, c, :], in0=z_banks[c][:], scalar=0.5, in1=half_bias[:], op0=ALU.mult, op1=ALU.add
+            )
+
+        def weigh(c):
+            nc.vector.tensor_tensor(
+                out=weighted[:, c],
+                in0=half_x[:, c, :].unsqueeze(1).to_broadcast([P, PERSP, JOINED]),
+                in1=w_all[:],
+                op=ALU.mult,
+            )
+            for p in range(PERSP):
+                nc.scalar.activation(
+                    out=squares[:], in_=weighted[:, c, p, :], func=ACT.Square, accum_out=norm_sq[:, c, p : p + 1]
                 )
-                nc.vector.tensor_tensor(out=weighted[:, c, 0, :], in0=half_x[:, c, :], in1=w_0[:], op=ALU.mult)
-                nc.gpsimd.tensor_tensor(out=weighted[:, c, 1, :], in0=half_x[:, c, :], in1=w_1[:], op=ALU.mult)
-                for p in range(PERSP):
-                    nc.scalar.activation(
-                        out=squares[:], in_=weighted[:, c, p, :], func=ACT.Square, accum_out=norm_sq[:, c, p : p + 1]
-                    )
-            nc.scalar.activation(out=norm[:, chunks, :], in_=norm_sq[:, chunks, :], func=ACT.Sqrt)
+            nc.scalar.activation(out=norm[:, c, :], in_=norm_sq[:, c, :], func=ACT.Sqrt)
 
+        def floor_norm(c):
+            nc.vector.tensor_scalar_max(out=norm_floor[:, c, :], in0=norm[:, c, :], scalar1=0.5 * EPS)
+
+        def invert_norm(c):
+            nc.vector.reciprocal(out=inv_norm[:, c, :], in_=norm_floor[:, c, :])
+
+        def normalise(c, p):
+            nc.vector.tensor_scalar_mul(
+                out=cf[:, c, p * JOINED : (p + 1) * JOINED], in0=weighted[:, c, p, :], scalar1=inv_norm[:, c, p : p + 1]
+            )
+
+        add_bias(0)
+        for c in range(CHUNKS):
+            if c + 1 < CHUNKS:
+                add_bias(c + 1)
+            if c == CHUNKS - 1:
+                floor_norm(0)
+            weigh(c)
+        invert_norm(0)
         cf_banks = []
-
-        def normalise_and_flip(pair):
-            chunks = slice(2 * pair, 2 * pair + 2)
-            nc.vector.tensor_scalar_max(out=norm_floor[:, chunks, :], in0=norm[:, chunks, :], scalar1=0.5 * EPS)
-            nc.vector.reciprocal(out=inv_norm[:, chunks, :], in_=norm_floor[:, chunks, :])
-            for c in (2 * pair, 2 * pair + 1):
-                for p in range(PERSP):
-                    nc.vector.tensor_scalar_mul(
-                        out=cf[:, c, p * JOINED : (p + 1) * JOINED],
-                        in0=weighted[:, c, p, :],
-                        scalar1=inv_norm[:, c, p : p + 1],
-                    )
-                cf_flipped = psum.tile([P, PACK, P], BF16, tag="stage%d" % c, name="cf_flipped")
-                for t in range(PACK):
-                    nc.tensor.transpose(cf_flipped[:, t, :], cf[:, c, t * P : (t + 1) * P], ident_bf16[:])
-                cf_banks.append(cf_flipped)
-
-        normalise_and_flip(0)
-        output = keep.tile([P, CHUNKS, FEAT], F32)
-        nc.vector.tensor_tensor(out=output[:], in0=half_x[:, :, 0:FEAT], in1=half_x[:, :, FEAT:JOINED], op=ALU.add)
-        nc.sync.dma_start(out=out_0.rearrange("(p c) f -> p c f", c=CHUNKS), in_=output[:])
-        normalise_and_flip(1)
+        for c in range(CHUNKS):
+            if c + 1 < CHUNKS:
+                floor_norm(c + 1)
+            normalise(c, 0)
+            if c + 1 < CHUNKS:
+                invert_norm(c + 1)
+            normalise(c, 1)
+            cf_flipped = psum.tile([P, PACK, P], BF16, tag="stage%d" % c, name="cf_flipped")
+            for t in range(PACK):
+                nc.tensor.transpose(cf_flipped[:, t, :], cf[:, c, t * P : (t + 1) * P], ident_bf16[:])
+            cf_banks.append(cf_flipped)
 
         for c in range(CHUNKS):
             copy = nc.vector.tensor_copy if c == CHUNKS - 2 else nc.scalar.copy
@@ -222,22 +229,25 @@ def tile_pmodel_pb_s_kernel(tc, adj1, hw, bg2, hm, Wm2, bm2, w_gl2, out_0, out_1
             )
             att_banks.append(att)
 
-        nc.vector.tensor_scalar_mul(out=half_adj[:, 2:4, :], in0=adj_sb[:, 2:4, :], scalar1=0.5)
+        output = keep.tile([P, CHUNKS, FEAT], F32)
+        nc.vector.tensor_tensor(out=output[:], in0=half_x[:, :, 0:FEAT], in1=half_x[:, :, FEAT:JOINED], op=ALU.add)
+        nc.sync.dma_start(out=out_0.rearrange("(c p) f -> p c f", p=P), in_=output[:])
+        nc.vector.tensor_scalar_mul(out=half_adj[:, 2, :], in0=adj_sb[:, 2, :], scalar1=0.5)
+        nc.scalar.mul(out=half_adj[:, 3, :], in_=adj_sb[:, 3, :], mul=0.5)
 
         masked = keep.tile([P, CHUNKS, NODES], F32)
         row_sum = keep.tile([P, CHUNKS], F32)
         twice_sum = keep.tile([P, CHUNKS], F32)
         half_inv_sum = keep.tile([P, CHUNKS], F32)
         adj = keep.tile([P, CHUNKS, NODES], F32)
-        adj_rows = out_1.rearrange("(p c) m -> p c m", c=CHUNKS)
-        for c in range(CHUNKS):
+        adj_rows = out_1.rearrange("(c p) m -> p c m", p=P)
+
+        def mask_and_sum(c):
             nc.scalar.activation(
-                out=masked[:, c, :].rearrange("n (j c) -> n j c", c=CHUNKS),
-                in_=att_banks[c][:].rearrange("n (c j) -> n j c", c=CHUNKS),
-                func=ACT.Relu,
-                scale=0.5,
-                accum_out=row_sum[:, c : c + 1],
+                out=masked[:, c, :], in_=att_banks[c][:], func=ACT.Relu, scale=0.5, accum_out=row_sum[:, c : c + 1]
             )
+
+        def floor_sum(c):
             nc.vector.tensor_scalar(
                 out=twice_sum[:, c : c + 1],
                 in0=row_sum[:, c : c + 1],
@@ -246,7 +256,17 @@ def tile_pmodel_pb_s_kernel(tc, adj1, hw, bg2, hm, Wm2, bm2, w_gl2, out_0, out_1
                 op0=ALU.max,
                 op1=ALU.mult,
             )
+
+        def invert_sum(c):
             nc.vector.reciprocal(out=half_inv_sum[:, c : c + 1], in_=twice_sum[:, c : c + 1])
+
+        for c in range(CHUNKS):
+            mask_and_sum(c)
+        floor_sum(0)
+        invert_sum(0)
+        for c in range(CHUNKS):
+            if c + 1 < CHUNKS:
+                floor_sum(c + 1)
             nc.vector.scalar_tensor_tensor(
                 out=adj[:, c, :],
                 in0=masked[:, c, :],
@@ -256,3 +276,5 @@ def tile_pmodel_pb_s_kernel(tc, adj1, hw, bg2, hm, Wm2, bm2, w_gl2, out_0, out_1
                 op1=ALU.add,
             )
             nc.sync.dma_start(out=adj_rows[:, c, :], in_=adj[:, c, :])
+            if c + 1 < CHUNKS:
+                invert_sum(c + 1)

@@ -16,6 +16,7 @@ PACK = 4
 NODES = 512
 CHUNKS = NODES // P
 PAIRS = CHUNKS // 2
+LAST = CHUNKS - 1
 FEAT = 128
 JOINED = 2 * FEAT
 PERSP = 2
@@ -50,7 +51,7 @@ def tile_pmodel_pb_s_kernel(tc, adj1, hw, bg2, hm, Wm2, bm2, w_gl2, out_0, out_1
         make_identity(nc, ident_bf16[:])
 
         def load_nodes(x_sb, x_dram):
-            rows = x_dram.rearrange("(c p) k -> p c k", p=P)
+            rows = x_dram.rearrange("(p c) k -> p c k", c=CHUNKS)
             for pair in range(PAIRS):
                 chunks = slice(2 * pair, 2 * pair + 2)
                 nc.sync.dma_start(out=x_sb[:, chunks, :], in_=rows[:, chunks, :])
@@ -206,7 +207,8 @@ def tile_pmodel_pb_s_kernel(tc, adj1, hw, bg2, hm, Wm2, bm2, w_gl2, out_0, out_1
         for c in range(CHUNKS):
             copy = nc.vector.tensor_copy if c == CHUNKS - 2 else nc.scalar.copy
             copy(out=cf_grouped[:, c], in_=cf_banks[c][:].rearrange("q t n -> q n t"))
-        for c in range(CHUNKS):
+
+        def quantise_cf(c):
             nodes = slice(c * P, (c + 1) * P)
             nc.vector.quantize_mx(
                 out=cf_codes[:, nodes].bitcast(FP8X4),
@@ -214,24 +216,37 @@ def tile_pmodel_pb_s_kernel(tc, adj1, hw, bg2, hm, Wm2, bm2, w_gl2, out_0, out_1
                 in_=cf_grouped[:, c].rearrange("q n t -> q (n t)"),
             )
 
-        att_banks = []
-        for c in range(CHUNKS):
+        def multiply_cf(att, c, first, count):
             nodes = slice(c * P, (c + 1) * P)
-            att = psum.tile([P, NODES], F32, tag="stage%d" % c, name="att")
+            others = slice(first * P, (first + count) * P)
             nc.tensor.matmul_mx(
-                out=att[:],
+                out=att[:, others],
                 lhsT=cf_codes[:, nodes].bitcast(FP8X4),
                 lhsT_scale=cf_scales[:, nodes],
-                rhs=cf_codes[:].bitcast(FP8X4),
-                rhs_scale=cf_scales[:],
+                rhs=cf_codes[:, others].bitcast(FP8X4),
+                rhs_scale=cf_scales[:, others],
                 start=True,
                 stop=True,
             )
+
+        att_banks = []
+        for c in range(LAST):
+            quantise_cf(c)
+        for c in range(LAST):
+            att = psum.tile([P, NODES], F32, tag="stage%d" % c, name="att")
+            multiply_cf(att, c, 0, 2)
+            multiply_cf(att, c, 2, 1)
             att_banks.append(att)
+        quantise_cf(LAST)
+        for c in range(LAST):
+            multiply_cf(att_banks[c], c, LAST, 1)
+        att = psum.tile([P, NODES], F32, tag="stage%d" % LAST, name="att")
+        multiply_cf(att, LAST, 0, CHUNKS)
+        att_banks.append(att)
 
         output = keep.tile([P, CHUNKS, FEAT], F32)
         nc.vector.tensor_tensor(out=output[:], in0=half_x[:, :, 0:FEAT], in1=half_x[:, :, FEAT:JOINED], op=ALU.add)
-        nc.sync.dma_start(out=out_0.rearrange("(c p) f -> p c f", p=P), in_=output[:])
+        nc.sync.dma_start(out=out_0.rearrange("(p c) f -> p c f", c=CHUNKS), in_=output[:])
         nc.vector.tensor_scalar_mul(out=half_adj[:, 2, :], in0=adj_sb[:, 2, :], scalar1=0.5)
         nc.scalar.mul(out=half_adj[:, 3, :], in_=adj_sb[:, 3, :], mul=0.5)
 
@@ -240,11 +255,15 @@ def tile_pmodel_pb_s_kernel(tc, adj1, hw, bg2, hm, Wm2, bm2, w_gl2, out_0, out_1
         twice_sum = keep.tile([P, CHUNKS], F32)
         half_inv_sum = keep.tile([P, CHUNKS], F32)
         adj = keep.tile([P, CHUNKS, NODES], F32)
-        adj_rows = out_1.rearrange("(c p) m -> p c m", p=P)
+        adj_rows = out_1.rearrange("(p c) m -> p c m", c=CHUNKS)
 
         def mask_and_sum(c):
             nc.scalar.activation(
-                out=masked[:, c, :], in_=att_banks[c][:], func=ACT.Relu, scale=0.5, accum_out=row_sum[:, c : c + 1]
+                out=masked[:, c, :].rearrange("n (j c) -> n j c", c=CHUNKS),
+                in_=att_banks[c][:].rearrange("n (c j) -> n j c", c=CHUNKS),
+                func=ACT.Relu,
+                scale=0.5,
+                accum_out=row_sum[:, c : c + 1],
             )
 
         def floor_sum(c):
@@ -260,6 +279,17 @@ def tile_pmodel_pb_s_kernel(tc, adj1, hw, bg2, hm, Wm2, bm2, w_gl2, out_0, out_1
         def invert_sum(c):
             nc.vector.reciprocal(out=half_inv_sum[:, c : c + 1], in_=twice_sum[:, c : c + 1])
 
+        def average(c, columns):
+            nc.vector.scalar_tensor_tensor(
+                out=adj[:, c, columns],
+                in0=masked[:, c, columns],
+                scalar=half_inv_sum[:, c : c + 1],
+                in1=half_adj[:, c, columns],
+                op0=ALU.mult,
+                op1=ALU.add,
+            )
+            nc.sync.dma_start(out=adj_rows[:, c, columns], in_=adj[:, c, columns])
+
         for c in range(CHUNKS):
             mask_and_sum(c)
         floor_sum(0)
@@ -267,14 +297,7 @@ def tile_pmodel_pb_s_kernel(tc, adj1, hw, bg2, hm, Wm2, bm2, w_gl2, out_0, out_1
         for c in range(CHUNKS):
             if c + 1 < CHUNKS:
                 floor_sum(c + 1)
-            nc.vector.scalar_tensor_tensor(
-                out=adj[:, c, :],
-                in0=masked[:, c, :],
-                scalar=half_inv_sum[:, c : c + 1],
-                in1=half_adj[:, c, :],
-                op0=ALU.mult,
-                op1=ALU.add,
-            )
-            nc.sync.dma_start(out=adj_rows[:, c, :], in_=adj[:, c, :])
+            average(c, slice(0, NODES // 2))
             if c + 1 < CHUNKS:
                 invert_sum(c + 1)
+            average(c, slice(NODES // 2, NODES))

@@ -16,13 +16,14 @@ PACK = 4
 NODES = 512
 CHUNKS = NODES // P
 PAIRS = CHUNKS // 2
+HALF = NODES // 2
 LAST = CHUNKS - 1
 FEAT = 128
-JOINED = 2 * FEAT
+PARTS = 2
 PERSP = 2
 EPS = 1e-12
 
-FLOPS = 2 * NODES * NODES * FEAT * 2 + 2 * NODES * NODES * PERSP * JOINED
+FLOPS = 2 * NODES * NODES * FEAT * 2 + 2 * NODES * NODES * PERSP * PARTS * FEAT
 
 
 def tile_pmodel_pb_s_kernel(tc, adj1, hw, bg2, hm, Wm2, bm2, w_gl2, out_0, out_1):
@@ -32,18 +33,29 @@ def tile_pmodel_pb_s_kernel(tc, adj1, hw, bg2, hm, Wm2, bm2, w_gl2, out_0, out_1
         psum = ctx.enter_context(tc.psum_pool(name="psum", bufs=1))
         ctx.enter_context(tc.manual_schedule())
 
-        w_row = keep.tile([P, PERSP * JOINED], BF16)
-        bias_row = keep.tile([P, JOINED], BF16)
-        ones = keep.tile([P, P], BF16)
+        warm_in = keep.tile([P, P], F32)
+        nc.vector.memset(warm_in[:], 1.0)
+        rows = keep.tile([P, FEAT], BF16)
+        pick_bias = keep.tile([P, P], BF16)
         one = keep.tile([P, 1], F32)
-        nc.vector.memset(w_row[:], 0.0)
-        nc.vector.memset(ones[:], 1.0)
+        nc.vector.memset(rows[:], 0.0)
         nc.vector.memset(one[:], 1.0)
-        nc.vector.memset(bias_row[:], 0.0)
-        nc.scalar.dma_start(out=w_row[0:1, :], in_=w_gl2.rearrange("(o p) f -> o (p f)", o=1))
+        nc.vector.memset(pick_bias[:], 0.0)
+        nc.vector.memset(pick_bias[0:2, :], 1.0)
+        nc.scalar.dma_start(out=rows[2:6, :], in_=w_gl2.rearrange("p (m f) -> (p m) f", m=PARTS))
+        nc.scalar.dma_start(out=rows[0:1, :], in_=bg2.rearrange("(o f) -> o f", o=1))
+        nc.scalar.dma_start(out=rows[1:2, :], in_=bm2.rearrange("(o f) -> o f", o=1))
 
         table_warm = keep.tile([P, 1], F32)
-        nc.scalar.activation(out=table_warm[:], in_=one[:], func=ACT.Sqrt)
+        nc.scalar.activation(out=table_warm[:], in_=one[:], func=ACT.Abs_reciprocal_sqrt)
+
+        warm_bank = psum.tile([P, P], F32, tag="z2v")
+
+        def keep_warm(count):
+            for i in range(count):
+                nc.tensor.matmul(out=warm_bank[:], lhsT=warm_in[:], rhs=warm_in[:], start=True, stop=True)
+
+        keep_warm(3)
 
         ident_f32 = keep.tile([P, P], F32)
         ident_bf16 = keep.tile([P, P], BF16)
@@ -51,14 +63,14 @@ def tile_pmodel_pb_s_kernel(tc, adj1, hw, bg2, hm, Wm2, bm2, w_gl2, out_0, out_1
         make_identity(nc, ident_bf16[:])
 
         def load_nodes(x_sb, x_dram):
-            rows = x_dram.rearrange("(p c) k -> p c k", c=CHUNKS)
+            x_rows = x_dram.rearrange("(p c) k -> p c k", c=CHUNKS)
             for pair in range(PAIRS):
                 chunks = slice(2 * pair, 2 * pair + 2)
-                nc.sync.dma_start(out=x_sb[:, chunks, :], in_=rows[:, chunks, :])
+                nc.sync.dma_start(out=x_sb[:, chunks, :], in_=x_rows[:, chunks, :])
 
         adj_sb = keep.tile([P, CHUNKS, NODES], BF16)
         hm_sb = keep.tile([P, CHUNKS, NODES], BF16)
-        weight_raw = keep.tile([P, 2, PACK, FEAT], BF16)
+        weight_raw = keep.tile([P, PARTS, PACK, FEAT], BF16)
         load_nodes(adj_sb, adj1)
         for m, weight in enumerate((hw, Wm2)):
             nc.sync.dma_start(
@@ -66,8 +78,6 @@ def tile_pmodel_pb_s_kernel(tc, adj1, hw, bg2, hm, Wm2, bm2, w_gl2, out_0, out_1
                 in_=weight.rearrange("(u q e) f -> q u e f", u=2, e=2),
             )
         load_nodes(hm_sb, hm)
-        nc.sync.dma_start(out=bias_row[0:1, 0:FEAT], in_=bg2.rearrange("(o f) -> o f", o=1))
-        nc.sync.dma_start(out=bias_row[0:1, FEAT:JOINED], in_=bm2.rearrange("(o f) -> o f", o=1))
 
         def make_operand(name):
             return {
@@ -76,137 +86,181 @@ def tile_pmodel_pb_s_kernel(tc, adj1, hw, bg2, hm, Wm2, bm2, w_gl2, out_0, out_1
                 "scales": keep.tile([P, NODES], U8, align_bytes=64, name=name + "_scales"),
             }
 
-        def flip_chunk(x_sb, operand, c, copy):
+        def flip_chunk(x_sb, c):
             words = x_sb[:].bitcast(F32)
             flipped = psum.tile([P, 2, P], F32, tag="stage%d" % c, name="flipped")
             for u in range(2):
                 nc.tensor.transpose(flipped[:, u, :], words[:, c, u * P : (u + 1) * P], ident_f32[:])
+            return flipped
+
+        def group_chunk(operand, c, flipped, copy):
             copy(out=operand["grouped"][:].bitcast(F32)[:, c], in_=flipped[:].rearrange("q u n -> q n u"))
 
         def quantise_pair(operand, pair):
-            nodes = slice(2 * pair * P, (2 * pair + 2) * P)
+            nodes = slice(pair * HALF, (pair + 1) * HALF)
             nc.vector.quantize_mx(
                 out=operand["codes"][:, nodes].bitcast(FP8X4),
                 scales=operand["scales"][:, nodes],
                 in_=operand["grouped"][:, 2 * pair : 2 * pair + 2].rearrange("q c n t -> q (c n t)"),
             )
 
+        weight_grouped = keep.tile([P, PARTS, FEAT, PACK], BF16, align_bytes=64)
+        weight_codes = keep.tile([P, PARTS, FEAT], U32, align_bytes=64)
+        weight_scales = keep.tile([P, PARTS, FEAT], U8, align_bytes=64)
+
+        def group_weight(m):
+            nc.scalar.copy(out=weight_grouped[:, m], in_=weight_raw[:, m].rearrange("q t f -> q f t"))
+
+        def quantise_weight(m):
+            nc.vector.quantize_mx(
+                out=weight_codes[:, m].bitcast(FP8X4),
+                scales=weight_scales[:, m],
+                in_=weight_grouped[:, m].rearrange("q f t -> q (f t)"),
+            )
+
         adj_mx = make_operand("adj")
-        for c in range(CHUNKS):
-            flip_chunk(adj_sb, adj_mx, c, nc.vector.tensor_copy)
-
-        w_spread = psum.tile([P, PERSP * JOINED], F32, tag="z0")
-        nc.tensor.matmul(out=w_spread[:], lhsT=ones[:], rhs=w_row[:], start=True, stop=True)
-        w_all = keep.tile([P, PERSP, JOINED], F32)
-        nc.scalar.copy(out=w_all[:].rearrange("n p f -> n (p f)"), in_=w_spread[:])
-
-        weight_grouped = keep.tile([P, 2, FEAT, PACK], BF16, align_bytes=64)
-        weight_codes = keep.tile([P, 2, FEAT], U32, align_bytes=64)
-        weight_scales = keep.tile([P, 2, FEAT], U8, align_bytes=64)
-        nc.vector.tensor_copy(out=weight_grouped[:], in_=weight_raw[:].rearrange("q m t f -> q m f t"))
-        for pair in range(PAIRS):
-            quantise_pair(adj_mx, pair)
-        nc.vector.quantize_mx(
-            out=weight_codes[:].rearrange("q m f -> q (m f)").bitcast(FP8X4),
-            scales=weight_scales[:].rearrange("q m f -> q (m f)"),
-            in_=weight_grouped[:].rearrange("q m f t -> q (m f t)"),
-        )
-
         hm_mx = make_operand("hm")
-        for pair in range(PAIRS):
-            flip_chunk(hm_sb, hm_mx, 2 * pair, nc.scalar.copy)
-            flip_chunk(hm_sb, hm_mx, 2 * pair + 1, nc.scalar.copy)
-            quantise_pair(hm_mx, pair)
-
-        bias_spread = psum.tile([P, JOINED], F32, tag="z3")
-        nc.tensor.matmul(out=bias_spread[:], lhsT=ones[:], rhs=bias_row[:], start=True, stop=True)
-        half_bias = keep.tile([P, JOINED], F32)
-        nc.scalar.activation(out=half_bias[:], in_=bias_spread[:], func=ACT.Copy, scale=0.5)
-
-        z_banks = []
         for c in range(CHUNKS):
-            nodes = slice(c * P, (c + 1) * P)
-            z = psum.tile([P, JOINED], F32, tag="z%d" % c, name="z")
-            for m, operand in enumerate((adj_mx, hm_mx)):
-                nc.tensor.matmul_mx(
-                    out=z[:, m * FEAT : (m + 1) * FEAT],
-                    lhsT=operand["codes"][:, nodes].bitcast(FP8X4),
-                    lhsT_scale=operand["scales"][:, nodes],
-                    rhs=weight_codes[:, m, :].bitcast(FP8X4),
-                    rhs_scale=weight_scales[:, m, :],
-                    start=True,
-                    stop=True,
+            group_chunk(adj_mx, c, flip_chunk(adj_sb, c), nc.vector.tensor_copy)
+        keep_warm(2)
+        group_weight(0)
+        group_weight(1)
+        quantise_pair(adj_mx, 0)
+        quantise_pair(adj_mx, 1)
+        quantise_weight(0)
+
+        hm_flipped = [flip_chunk(hm_sb, c) for c in (0, 1)]
+        group_chunk(hm_mx, 0, hm_flipped[0], nc.scalar.copy)
+        group_chunk(hm_mx, 1, hm_flipped[1], nc.vector.tensor_copy)
+
+        vector_bank = psum.tile([P, P], BF16, tag="z2s")
+        nc.tensor.transpose(vector_bank[:], rows[:], ident_bf16[:])
+        vectors = keep.tile([P, PARTS + PERSP * PARTS], F32)
+        weight_sq = keep.tile([P, PARTS, PERSP], F32)
+        nc.vector.tensor_copy(out=vectors[:], in_=vector_bank[:, 0 : PARTS + PERSP * PARTS])
+        quantise_weight(1)
+
+        hm_flipped += [flip_chunk(hm_sb, c) for c in (2, 3)]
+        group_chunk(hm_mx, 2, hm_flipped[2], nc.scalar.copy)
+        quantise_pair(hm_mx, 0)
+        group_chunk(hm_mx, 3, hm_flipped[3], nc.vector.tensor_copy)
+
+        def bias_column(m):
+            return vectors[:, m : m + 1]
+
+        def weight_column(p, m):
+            j = PARTS + PARTS * p + m
+            return vectors[:, j : j + 1]
+
+        weight_columns = vectors[:, PARTS : PARTS + PERSP * PARTS].rearrange("f (p m) -> f m p", m=PARTS)
+        nc.vector.tensor_tensor(out=weight_sq[:], in0=weight_columns, in1=weight_columns, op=ALU.mult)
+        quantise_pair(hm_mx, 1)
+
+        def multiply_z(bank, m, operand, nodes):
+            nc.tensor.matmul_mx(
+                out=bank[:, nodes],
+                lhsT=weight_codes[:, m, :].bitcast(FP8X4),
+                lhsT_scale=weight_scales[:, m, :],
+                rhs=operand["codes"][:, nodes].bitcast(FP8X4),
+                rhs_scale=operand["scales"][:, nodes],
+                start=True,
+                stop=True,
+            )
+
+        z1_s = psum.tile([P, NODES], F32, tag="z1s")
+        z1_v = psum.tile([P, NODES], F32, tag="z1v")
+        z2_s = psum.tile([P, NODES], F32, tag="z2s")
+        z2_v = psum.tile([P, NODES], F32, tag="z2v")
+        multiply_z(z1_s, 0, adj_mx, slice(0, NODES))
+        multiply_z(z1_v, 0, adj_mx, slice(0, NODES))
+        pair_nodes = [slice(pair * HALF, (pair + 1) * HALF) for pair in range(PAIRS)]
+        multiply_z(z2_s, 1, hm_mx, pair_nodes[0])
+        multiply_z(z2_v, 1, hm_mx, pair_nodes[0])
+
+        squares = keep.tile([P, PARTS, NODES], F32)
+        weighted = keep.tile([P, PERSP, PARTS, NODES], F32)
+        nc.scalar.activation(out=squares[:, 0, :], in_=z1_s[:], func=ACT.Square, bias=bias_column(0))
+
+        norm_banks = [
+            psum.tile([P, 2, PERSP], F32, tag="stage%d" % pair, name="norm_bank") for pair in range(PAIRS)
+        ]
+
+        def sum_squares(m, pair):
+            for j in range(2):
+                c = 2 * pair + j
+                nc.tensor.matmul(
+                    out=norm_banks[pair][:, j, :],
+                    lhsT=squares[:, m, c * P : (c + 1) * P],
+                    rhs=weight_sq[:, m, :],
+                    start=(m == 0 and j == 0),
+                    stop=(m == PARTS - 1 and j == 1),
                 )
-            z_banks.append(z)
 
-        half_adj = keep.tile([P, CHUNKS, NODES], BF16)
-        nc.scalar.mul(out=half_adj[:, 0:2, :], in_=adj_sb[:, 0:2, :], mul=0.5)
+        def square_z2(nodes):
+            nc.scalar.activation(out=squares[:, 1, nodes], in_=z2_s[:, nodes], func=ACT.Square, bias=bias_column(1))
 
-        half_x = keep.tile([P, CHUNKS, JOINED], F32)
-        weighted = keep.tile([P, CHUNKS, PERSP, JOINED], F32)
-        squares = keep.tile([P, JOINED], BF16)
-        norm_sq = keep.tile([P, CHUNKS, PERSP], F32)
-        norm = keep.tile([P, CHUNKS, PERSP], F32)
+        square_z2(pair_nodes[0])
+        for pair in range(PAIRS):
+            sum_squares(0, pair)
+        multiply_z(z2_s, 1, hm_mx, pair_nodes[1])
+        multiply_z(z2_v, 1, hm_mx, pair_nodes[1])
+        square_z2(pair_nodes[1])
+        for pair in range(PAIRS):
+            sum_squares(1, pair)
+
         norm_floor = keep.tile([P, CHUNKS, PERSP], F32)
         inv_norm = keep.tile([P, CHUNKS, PERSP], F32)
-        cf = keep.tile([P, CHUNKS, PERSP * JOINED], BF16)
+
+        def weigh(p, m, z, nodes):
+            nc.vector.tensor_scalar(
+                out=weighted[:, p, m, nodes],
+                in0=z[:, nodes],
+                scalar1=bias_column(m),
+                scalar2=weight_column(p, m),
+                op0=ALU.add,
+                op1=ALU.mult,
+            )
+
+        def invert_norms(pair):
+            chunks = slice(2 * pair, 2 * pair + 2)
+            nc.vector.tensor_scalar_max(out=norm_floor[:, chunks, :], in0=norm_banks[pair][:], scalar1=EPS * EPS)
+            nc.scalar.activation(
+                out=inv_norm[:, chunks, :], in_=norm_floor[:, chunks, :], func=ACT.Abs_reciprocal_sqrt
+            )
+
+        spread_banks = []
+
+        def spread_norms(pair):
+            bank = psum.tile([P, 2, PERSP, P], F32, tag="stage%d" % (2 + pair), name="spread_bank")
+            for j in range(2):
+                for p in range(PERSP):
+                    column = inv_norm[:, 2 * pair + j, p : p + 1]
+                    nc.tensor.transpose(bank[:, j, p, :], column.to_broadcast([P, P]), ident_f32[:])
+            spread_banks.append(bank)
+
+        for p in range(PERSP):
+            weigh(p, 0, z1_v, slice(0, NODES))
+        for p in range(PERSP):
+            weigh(p, 1, z2_v, pair_nodes[0])
+        invert_norms(0)
+        spread_norms(0)
+        for p in range(PERSP):
+            weigh(p, 1, z2_v, pair_nodes[1])
+        invert_norms(1)
+        spread_norms(1)
+
         cf_grouped = keep.tile([P, CHUNKS, P, PACK], BF16, align_bytes=64)
         cf_codes = keep.tile([P, NODES], U32, align_bytes=64)
         cf_scales = keep.tile([P, NODES], U8, align_bytes=64)
 
-        def add_bias(c):
-            nc.vector.scalar_tensor_tensor(
-                out=half_x[:, c, :], in0=z_banks[c][:], scalar=0.5, in1=half_bias[:], op0=ALU.mult, op1=ALU.add
-            )
-
-        def weigh(c):
+        def normalise(c):
+            pair, j = divmod(c, 2)
             nc.vector.tensor_tensor(
-                out=weighted[:, c],
-                in0=half_x[:, c, :].unsqueeze(1).to_broadcast([P, PERSP, JOINED]),
-                in1=w_all[:],
+                out=cf_grouped[:, c].rearrange("q n (p m) -> q n p m", m=PARTS),
+                in0=weighted[:, :, :, c * P : (c + 1) * P].rearrange("q p m n -> q n p m"),
+                in1=spread_banks[pair][:, j].rearrange("q p n -> q n p").unsqueeze(3).to_broadcast([P, P, PERSP, PARTS]),
                 op=ALU.mult,
             )
-            for p in range(PERSP):
-                nc.scalar.activation(
-                    out=squares[:], in_=weighted[:, c, p, :], func=ACT.Square, accum_out=norm_sq[:, c, p : p + 1]
-                )
-            nc.scalar.activation(out=norm[:, c, :], in_=norm_sq[:, c, :], func=ACT.Sqrt)
-
-        def floor_norm(c):
-            nc.vector.tensor_scalar_max(out=norm_floor[:, c, :], in0=norm[:, c, :], scalar1=0.5 * EPS)
-
-        def invert_norm(c):
-            nc.vector.reciprocal(out=inv_norm[:, c, :], in_=norm_floor[:, c, :])
-
-        def normalise(c, p):
-            nc.vector.tensor_scalar_mul(
-                out=cf[:, c, p * JOINED : (p + 1) * JOINED], in0=weighted[:, c, p, :], scalar1=inv_norm[:, c, p : p + 1]
-            )
-
-        add_bias(0)
-        for c in range(CHUNKS):
-            if c + 1 < CHUNKS:
-                add_bias(c + 1)
-            if c == CHUNKS - 1:
-                floor_norm(0)
-            weigh(c)
-        invert_norm(0)
-        cf_banks = []
-        for c in range(CHUNKS):
-            if c + 1 < CHUNKS:
-                floor_norm(c + 1)
-            normalise(c, 0)
-            if c + 1 < CHUNKS:
-                invert_norm(c + 1)
-            normalise(c, 1)
-            cf_flipped = psum.tile([P, PACK, P], BF16, tag="stage%d" % c, name="cf_flipped")
-            for t in range(PACK):
-                nc.tensor.transpose(cf_flipped[:, t, :], cf[:, c, t * P : (t + 1) * P], ident_bf16[:])
-            cf_banks.append(cf_flipped)
-
-        for c in range(CHUNKS):
-            copy = nc.vector.tensor_copy if c == CHUNKS - 2 else nc.scalar.copy
-            copy(out=cf_grouped[:, c], in_=cf_banks[c][:].rearrange("q t n -> q n t"))
 
         def quantise_cf(c):
             nodes = slice(c * P, (c + 1) * P)
@@ -215,6 +269,45 @@ def tile_pmodel_pb_s_kernel(tc, adj1, hw, bg2, hm, Wm2, bm2, w_gl2, out_0, out_1
                 scales=cf_scales[:, nodes],
                 in_=cf_grouped[:, c].rearrange("q n t -> q (n t)"),
             )
+
+        normalise(0)
+        for c in range(1, CHUNKS):
+            normalise(c)
+            quantise_cf(c - 1)
+        quantise_cf(LAST)
+
+        bias_bank = psum.tile([P, FEAT], F32, tag="z1s")
+        nc.tensor.matmul(out=bias_bank[:], lhsT=pick_bias[:], rhs=rows[:], start=True, stop=True)
+        half_bias = keep.tile([P, FEAT], F32)
+        nc.scalar.activation(out=half_bias[:], in_=bias_bank[:], func=ACT.Copy, scale=0.5)
+        sum_bank = psum.tile([P, CHUNKS, FEAT], F32, tag="z1v")
+        for c in range(CHUNKS):
+            nodes = slice(c * P, (c + 1) * P)
+            for m, operand in enumerate((adj_mx, hm_mx)):
+                nc.tensor.matmul_mx(
+                    out=sum_bank[:, c, :],
+                    lhsT=operand["codes"][:, nodes].bitcast(FP8X4),
+                    lhsT_scale=operand["scales"][:, nodes],
+                    rhs=weight_codes[:, m, :].bitcast(FP8X4),
+                    rhs_scale=weight_scales[:, m, :],
+                    start=(m == 0),
+                    stop=(m == PARTS - 1),
+                )
+        output = keep.tile([P, CHUNKS, FEAT], F32)
+        nc.vector.scalar_tensor_tensor(
+            out=output[:],
+            in0=sum_bank[:],
+            scalar=0.5,
+            in1=half_bias[:].unsqueeze(1).to_broadcast([P, CHUNKS, FEAT]),
+            op0=ALU.mult,
+            op1=ALU.add,
+        )
+        nc.sync.dma_start(out=out_0.rearrange("(p c) f -> p c f", c=CHUNKS), in_=output[:])
+
+        half_adj = keep.tile([P, CHUNKS, NODES], BF16)
+        for pair in range(PAIRS):
+            chunks = slice(2 * pair, 2 * pair + 2)
+            nc.scalar.mul(out=half_adj[:, chunks, :], in_=adj_sb[:, chunks, :], mul=0.5)
 
         def multiply_cf(att, c, first, count):
             nodes = slice(c * P, (c + 1) * P)
@@ -230,25 +323,14 @@ def tile_pmodel_pb_s_kernel(tc, adj1, hw, bg2, hm, Wm2, bm2, w_gl2, out_0, out_1
             )
 
         att_banks = []
+        for c, tag in enumerate(("stage0", "stage1", "z1s", "z2s")):
+            att_banks.append(psum.tile([P, NODES], F32, tag=tag, name="att"))
         for c in range(LAST):
-            quantise_cf(c)
-        for c in range(LAST):
-            att = psum.tile([P, NODES], F32, tag="stage%d" % c, name="att")
-            multiply_cf(att, c, 0, 2)
-            multiply_cf(att, c, 2, 1)
-            att_banks.append(att)
-        quantise_cf(LAST)
+            multiply_cf(att_banks[c], c, 0, 2)
+            multiply_cf(att_banks[c], c, 2, 1)
         for c in range(LAST):
             multiply_cf(att_banks[c], c, LAST, 1)
-        att = psum.tile([P, NODES], F32, tag="stage%d" % LAST, name="att")
-        multiply_cf(att, LAST, 0, CHUNKS)
-        att_banks.append(att)
-
-        output = keep.tile([P, CHUNKS, FEAT], F32)
-        nc.vector.tensor_tensor(out=output[:], in0=half_x[:, :, 0:FEAT], in1=half_x[:, :, FEAT:JOINED], op=ALU.add)
-        nc.sync.dma_start(out=out_0.rearrange("(p c) f -> p c f", c=CHUNKS), in_=output[:])
-        nc.vector.tensor_scalar_mul(out=half_adj[:, 2, :], in0=adj_sb[:, 2, :], scalar1=0.5)
-        nc.scalar.mul(out=half_adj[:, 3, :], in_=adj_sb[:, 3, :], mul=0.5)
+        multiply_cf(att_banks[LAST], LAST, 0, CHUNKS)
 
         masked = keep.tile([P, CHUNKS, NODES], F32)
         row_sum = keep.tile([P, CHUNKS], F32)

@@ -34,11 +34,11 @@ def tile_pmodel_pb_s_kernel(tc, adj1, hw, bg2, hm, Wm2, bm2, w_gl2, out_0, out_1
         ctx.enter_context(tc.manual_schedule())
 
         warm_in = keep.tile([P, P], F32)
-        nc.vector.memset(warm_in[:], 1.0)
         rows = keep.tile([P, FEAT], BF16)
         pick_bias = keep.tile([P, P], BF16)
         one = keep.tile([P, 1], F32)
         nc.vector.memset(rows[:], 0.0)
+        nc.vector.memset(warm_in[:], 1.0)
         nc.vector.memset(one[:], 1.0)
         nc.vector.memset(pick_bias[:], 0.0)
         nc.vector.memset(pick_bias[0:2, :], 1.0)
@@ -49,13 +49,11 @@ def tile_pmodel_pb_s_kernel(tc, adj1, hw, bg2, hm, Wm2, bm2, w_gl2, out_0, out_1
         table_warm = keep.tile([P, 1], F32)
         nc.scalar.activation(out=table_warm[:], in_=one[:], func=ACT.Abs_reciprocal_sqrt)
 
-        warm_bank = psum.tile([P, P], F32, tag="z2v")
+        warm_bank = psum.tile([P, P], F32, tag="bank7")
 
         def keep_warm(count):
             for i in range(count):
                 nc.tensor.matmul(out=warm_bank[:], lhsT=warm_in[:], rhs=warm_in[:], start=True, stop=True)
-
-        keep_warm(3)
 
         ident_f32 = keep.tile([P, P], F32)
         ident_bf16 = keep.tile([P, P], BF16)
@@ -63,10 +61,9 @@ def tile_pmodel_pb_s_kernel(tc, adj1, hw, bg2, hm, Wm2, bm2, w_gl2, out_0, out_1
         make_identity(nc, ident_bf16[:])
 
         def load_nodes(x_sb, x_dram):
-            x_rows = x_dram.rearrange("(p c) k -> p c k", c=CHUNKS)
+            x_rows = x_dram.rearrange("(h q j) k -> h q j k", h=PAIRS, j=2)
             for pair in range(PAIRS):
-                chunks = slice(2 * pair, 2 * pair + 2)
-                nc.sync.dma_start(out=x_sb[:, chunks, :], in_=x_rows[:, chunks, :])
+                nc.sync.dma_start(out=x_sb[:, 2 * pair : 2 * pair + 2, :], in_=x_rows[pair])
 
         adj_sb = keep.tile([P, CHUNKS, NODES], BF16)
         hm_sb = keep.tile([P, CHUNKS, NODES], BF16)
@@ -118,32 +115,31 @@ def tile_pmodel_pb_s_kernel(tc, adj1, hw, bg2, hm, Wm2, bm2, w_gl2, out_0, out_1
                 in_=weight_grouped[:, m].rearrange("q f t -> q (f t)"),
             )
 
+        vector_copy = nc.vector.tensor_copy
+        scalar_copy = nc.scalar.copy
         adj_mx = make_operand("adj")
         hm_mx = make_operand("hm")
-        for c in range(CHUNKS):
-            group_chunk(adj_mx, c, flip_chunk(adj_sb, c), nc.vector.tensor_copy)
-        keep_warm(2)
+        keep_warm(3)
+        for c, copy in enumerate((scalar_copy, vector_copy, vector_copy, vector_copy)):
+            group_chunk(adj_mx, c, flip_chunk(adj_sb, c), copy)
+        keep_warm(3)
         group_weight(0)
         group_weight(1)
         quantise_pair(adj_mx, 0)
         quantise_pair(adj_mx, 1)
         quantise_weight(0)
-
         hm_flipped = [flip_chunk(hm_sb, c) for c in (0, 1)]
-        group_chunk(hm_mx, 0, hm_flipped[0], nc.scalar.copy)
-        group_chunk(hm_mx, 1, hm_flipped[1], nc.vector.tensor_copy)
 
-        vector_bank = psum.tile([P, P], BF16, tag="z2s")
+        vector_bank = psum.tile([P, P], BF16, tag="bank5")
         nc.tensor.transpose(vector_bank[:], rows[:], ident_bf16[:])
+        bias_bank = psum.tile([P, FEAT], F32, tag="bank6")
+        nc.tensor.matmul(out=bias_bank[:], lhsT=pick_bias[:], rhs=rows[:], start=True, stop=True)
+        hm_flipped += [flip_chunk(hm_sb, c) for c in (2, 3)]
         vectors = keep.tile([P, PARTS + PERSP * PARTS], F32)
         weight_sq = keep.tile([P, PARTS, PERSP], F32)
-        nc.vector.tensor_copy(out=vectors[:], in_=vector_bank[:, 0 : PARTS + PERSP * PARTS])
-        quantise_weight(1)
-
-        hm_flipped += [flip_chunk(hm_sb, c) for c in (2, 3)]
-        group_chunk(hm_mx, 2, hm_flipped[2], nc.scalar.copy)
-        quantise_pair(hm_mx, 0)
-        group_chunk(hm_mx, 3, hm_flipped[3], nc.vector.tensor_copy)
+        weight_bias = keep.tile([P, PERSP], F32)
+        half_bias = keep.tile([P, FEAT], F32)
+        weight_columns = vectors[:, PARTS : PARTS + PERSP * PARTS].rearrange("f (p m) -> f m p", m=PARTS)
 
         def bias_column(m):
             return vectors[:, m : m + 1]
@@ -152,13 +148,22 @@ def tile_pmodel_pb_s_kernel(tc, adj1, hw, bg2, hm, Wm2, bm2, w_gl2, out_0, out_1
             j = PARTS + PARTS * p + m
             return vectors[:, j : j + 1]
 
-        weight_columns = vectors[:, PARTS : PARTS + PERSP * PARTS].rearrange("f (p m) -> f m p", m=PARTS)
+        group_chunk(hm_mx, 0, hm_flipped[0], scalar_copy)
+        nc.scalar.activation(out=half_bias[:], in_=bias_bank[:], func=ACT.Copy, scale=0.5)
+        nc.vector.tensor_copy(out=vectors[:], in_=vector_bank[:, 0 : PARTS + PERSP * PARTS])
+        group_chunk(hm_mx, 1, hm_flipped[1], vector_copy)
+        quantise_weight(1)
+        quantise_pair(hm_mx, 0)
         nc.vector.tensor_tensor(out=weight_sq[:], in0=weight_columns, in1=weight_columns, op=ALU.mult)
+        group_chunk(hm_mx, 2, hm_flipped[2], scalar_copy)
+        group_chunk(hm_mx, 3, hm_flipped[3], vector_copy)
+        nc.vector.tensor_scalar_mul(out=weight_bias[:], in0=weight_columns[:, 0, :], scalar1=bias_column(0))
         quantise_pair(hm_mx, 1)
 
-        def multiply_z(bank, m, operand, nodes):
+        def multiply_z(tag, m, operand, nodes):
+            bank = psum.tile([P, nodes.stop - nodes.start], F32, tag=tag, name="z")
             nc.tensor.matmul_mx(
-                out=bank[:, nodes],
+                out=bank[:],
                 lhsT=weight_codes[:, m, :].bitcast(FP8X4),
                 lhsT_scale=weight_scales[:, m, :],
                 rhs=operand["codes"][:, nodes].bitcast(FP8X4),
@@ -166,24 +171,36 @@ def tile_pmodel_pb_s_kernel(tc, adj1, hw, bg2, hm, Wm2, bm2, w_gl2, out_0, out_1
                 start=True,
                 stop=True,
             )
-
-        z1_s = psum.tile([P, NODES], F32, tag="z1s")
-        z1_v = psum.tile([P, NODES], F32, tag="z1v")
-        z2_s = psum.tile([P, NODES], F32, tag="z2s")
-        z2_v = psum.tile([P, NODES], F32, tag="z2v")
-        multiply_z(z1_s, 0, adj_mx, slice(0, NODES))
-        multiply_z(z1_v, 0, adj_mx, slice(0, NODES))
-        pair_nodes = [slice(pair * HALF, (pair + 1) * HALF) for pair in range(PAIRS)]
-        multiply_z(z2_s, 1, hm_mx, pair_nodes[0])
-        multiply_z(z2_v, 1, hm_mx, pair_nodes[0])
+            return bank
 
         squares = keep.tile([P, PARTS, NODES], F32)
         weighted = keep.tile([P, PERSP, PARTS, NODES], F32)
-        nc.scalar.activation(out=squares[:, 0, :], in_=z1_s[:], func=ACT.Square, bias=bias_column(0))
+        norm_floor = keep.tile([P, CHUNKS, PERSP], F32)
+        inv_norm = keep.tile([P, CHUNKS, PERSP], F32)
+        all_nodes = slice(0, NODES)
+        pair_nodes = [slice(pair * HALF, (pair + 1) * HALF) for pair in range(PAIRS)]
 
-        norm_banks = [
-            psum.tile([P, 2, PERSP], F32, tag="stage%d" % pair, name="norm_bank") for pair in range(PAIRS)
-        ]
+        def square(m, z, nodes):
+            nc.scalar.activation(out=squares[:, m, nodes], in_=z[:], func=ACT.Square, bias=bias_column(m))
+
+        def weigh_z1(p):
+            nc.scalar.activation(
+                out=weighted[:, p, 0, :],
+                in_=z1[:],
+                func=ACT.Identity,
+                scale=weight_column(p, 0),
+                bias=weight_bias[:, p : p + 1],
+            )
+
+        def weigh_z2(p, pair):
+            nc.vector.tensor_scalar(
+                out=weighted[:, p, 1, pair_nodes[pair]],
+                in0=z2_v[pair][:],
+                scalar1=bias_column(1),
+                scalar2=weight_column(p, 1),
+                op0=ALU.add,
+                op1=ALU.mult,
+            )
 
         def sum_squares(m, pair):
             for j in range(2):
@@ -196,31 +213,6 @@ def tile_pmodel_pb_s_kernel(tc, adj1, hw, bg2, hm, Wm2, bm2, w_gl2, out_0, out_1
                     stop=(m == PARTS - 1 and j == 1),
                 )
 
-        def square_z2(nodes):
-            nc.scalar.activation(out=squares[:, 1, nodes], in_=z2_s[:, nodes], func=ACT.Square, bias=bias_column(1))
-
-        square_z2(pair_nodes[0])
-        for pair in range(PAIRS):
-            sum_squares(0, pair)
-        multiply_z(z2_s, 1, hm_mx, pair_nodes[1])
-        multiply_z(z2_v, 1, hm_mx, pair_nodes[1])
-        square_z2(pair_nodes[1])
-        for pair in range(PAIRS):
-            sum_squares(1, pair)
-
-        norm_floor = keep.tile([P, CHUNKS, PERSP], F32)
-        inv_norm = keep.tile([P, CHUNKS, PERSP], F32)
-
-        def weigh(p, m, z, nodes):
-            nc.vector.tensor_scalar(
-                out=weighted[:, p, m, nodes],
-                in0=z[:, nodes],
-                scalar1=bias_column(m),
-                scalar2=weight_column(p, m),
-                op0=ALU.add,
-                op1=ALU.mult,
-            )
-
         def invert_norms(pair):
             chunks = slice(2 * pair, 2 * pair + 2)
             nc.vector.tensor_scalar_max(out=norm_floor[:, chunks, :], in0=norm_banks[pair][:], scalar1=EPS * EPS)
@@ -230,57 +222,39 @@ def tile_pmodel_pb_s_kernel(tc, adj1, hw, bg2, hm, Wm2, bm2, w_gl2, out_0, out_1
 
         spread_banks = []
 
-        def spread_norms(pair):
-            bank = psum.tile([P, 2, PERSP, P], F32, tag="stage%d" % (2 + pair), name="spread_bank")
-            for j in range(2):
-                for p in range(PERSP):
-                    column = inv_norm[:, 2 * pair + j, p : p + 1]
-                    nc.tensor.transpose(bank[:, j, p, :], column.to_broadcast([P, P]), ident_f32[:])
+        def spread_norms(c, tag):
+            bank = psum.tile([P, PERSP, P], F32, tag=tag, name="spread_bank")
+            for p in range(PERSP):
+                nc.tensor.transpose(bank[:, p, :], inv_norm[:, c, p : p + 1].to_broadcast([P, P]), ident_f32[:])
             spread_banks.append(bank)
 
+        z1 = multiply_z("bank4", 0, adj_mx, all_nodes)
+        square(0, z1, all_nodes)
+        for i in range(2):
+            multiply_z("bank5", 0, adj_mx, all_nodes)
+        z2_s = [multiply_z("bank6", 1, hm_mx, pair_nodes[0])]
+        z2_v = [multiply_z("bank7", 1, hm_mx, pair_nodes[0])]
+        square(1, z2_s[0], pair_nodes[0])
+        norm_banks = [
+            psum.tile([P, 2, PERSP], F32, tag="stage%d" % pair, name="norm_bank") for pair in range(PAIRS)
+        ]
+        sum_squares(0, 0)
+        sum_squares(1, 0)
+        z2_s.append(multiply_z("stage2", 1, hm_mx, pair_nodes[1]))
+        z2_v.append(multiply_z("stage3", 1, hm_mx, pair_nodes[1]))
         for p in range(PERSP):
-            weigh(p, 0, z1_v, slice(0, NODES))
+            weigh_z1(p)
         for p in range(PERSP):
-            weigh(p, 1, z2_v, pair_nodes[0])
+            weigh_z2(p, 0)
+        sum_squares(0, 1)
+
         invert_norms(0)
-        spread_norms(0)
-        for p in range(PERSP):
-            weigh(p, 1, z2_v, pair_nodes[1])
-        invert_norms(1)
-        spread_norms(1)
+        for c in (0, 1):
+            spread_norms(c, ("bank5", "bank7")[c])
+        square(1, z2_s[1], pair_nodes[1])
+        sum_squares(1, 1)
 
-        cf_grouped = keep.tile([P, CHUNKS, P, PACK], BF16, align_bytes=64)
-        cf_codes = keep.tile([P, NODES], U32, align_bytes=64)
-        cf_scales = keep.tile([P, NODES], U8, align_bytes=64)
-
-        def normalise(c):
-            pair, j = divmod(c, 2)
-            nc.vector.tensor_tensor(
-                out=cf_grouped[:, c].rearrange("q n (p m) -> q n p m", m=PARTS),
-                in0=weighted[:, :, :, c * P : (c + 1) * P].rearrange("q p m n -> q n p m"),
-                in1=spread_banks[pair][:, j].rearrange("q p n -> q n p").unsqueeze(3).to_broadcast([P, P, PERSP, PARTS]),
-                op=ALU.mult,
-            )
-
-        def quantise_cf(c):
-            nodes = slice(c * P, (c + 1) * P)
-            nc.vector.quantize_mx(
-                out=cf_codes[:, nodes].bitcast(FP8X4),
-                scales=cf_scales[:, nodes],
-                in_=cf_grouped[:, c].rearrange("q n t -> q (n t)"),
-            )
-
-        normalise(0)
-        for c in range(1, CHUNKS):
-            normalise(c)
-            quantise_cf(c - 1)
-        quantise_cf(LAST)
-
-        bias_bank = psum.tile([P, FEAT], F32, tag="z1s")
-        nc.tensor.matmul(out=bias_bank[:], lhsT=pick_bias[:], rhs=rows[:], start=True, stop=True)
-        half_bias = keep.tile([P, FEAT], F32)
-        nc.scalar.activation(out=half_bias[:], in_=bias_bank[:], func=ACT.Copy, scale=0.5)
-        sum_bank = psum.tile([P, CHUNKS, FEAT], F32, tag="z1v")
+        sum_bank = psum.tile([P, CHUNKS, FEAT], F32, tag="bank6")
         for c in range(CHUNKS):
             nodes = slice(c * P, (c + 1) * P)
             for m, operand in enumerate((adj_mx, hm_mx)):
@@ -293,6 +267,95 @@ def tile_pmodel_pb_s_kernel(tc, adj1, hw, bg2, hm, Wm2, bm2, w_gl2, out_0, out_1
                     start=(m == 0),
                     stop=(m == PARTS - 1),
                 )
+
+        half_adj = keep.tile([P, CHUNKS, NODES], BF16)
+
+        def halve_adj(c):
+            nc.scalar.mul(out=half_adj[:, c, :], in_=adj_sb[:, c, :], mul=0.5)
+
+        halve_adj(0)
+        halve_adj(1)
+        for p in range(PERSP):
+            weigh_z2(p, 1)
+
+        cf_grouped = keep.tile([P, CHUNKS, P, PACK], BF16, align_bytes=64)
+        cf_codes = keep.tile([P, NODES], U32, align_bytes=64)
+        cf_scales = keep.tile([P, NODES], U8, align_bytes=64)
+
+        def normalise(c):
+            nc.vector.tensor_tensor(
+                out=cf_grouped[:, c].rearrange("q n (p m) -> q n p m", m=PARTS),
+                in0=weighted[:, :, :, c * P : (c + 1) * P].rearrange("q p m n -> q n p m"),
+                in1=spread_banks[c][:].rearrange("q p n -> q n p").unsqueeze(3).to_broadcast([P, P, PERSP, PARTS]),
+                op=ALU.mult,
+            )
+
+        def quantise_cf(c):
+            nodes = slice(c * P, (c + 1) * P)
+            nc.vector.quantize_mx(
+                out=cf_codes[:, nodes].bitcast(FP8X4),
+                scales=cf_scales[:, nodes],
+                in_=cf_grouped[:, c].rearrange("q n t -> q (n t)"),
+            )
+
+        att_banks = [
+            psum.tile([P, NODES], F32, tag=tag, name="att") for tag in ("bank4", "stage1", "stage2", "bank5")
+        ]
+
+        def multiply_cf(c, first, count):
+            nodes = slice(c * P, (c + 1) * P)
+            others = slice(first * P, (first + count) * P)
+            nc.tensor.matmul_mx(
+                out=att_banks[c][:, others],
+                lhsT=cf_codes[:, nodes].bitcast(FP8X4),
+                lhsT_scale=cf_scales[:, nodes],
+                rhs=cf_codes[:, others].bitcast(FP8X4),
+                rhs_scale=cf_scales[:, others],
+                start=True,
+                stop=True,
+            )
+
+        masked = keep.tile([P, CHUNKS, NODES], F32)
+        row_sum = keep.tile([P, CHUNKS], F32)
+        twice_sum = keep.tile([P, CHUNKS], F32)
+        half_inv_sum = keep.tile([P, CHUNKS], F32)
+        adj = keep.tile([P, CHUNKS, NODES], F32)
+        adj_rows = out_1.rearrange("(h q j) m -> h q j m", h=PAIRS, j=2)
+
+        def mask_and_sum(c):
+            nc.scalar.activation(
+                out=masked[:, c, :].rearrange("n (h q j) -> n h q j", h=PAIRS, j=2),
+                in_=att_banks[c][:].rearrange("n (h j q) -> n h q j", h=PAIRS, j=2),
+                func=ACT.Relu,
+                accum_out=row_sum[:, c : c + 1],
+            )
+
+        normalise(0)
+        invert_norms(1)
+        halve_adj(2)
+        halve_adj(3)
+        for c in (2, 3):
+            spread_norms(c, ("stage0", "stage3")[c - 2])
+        for i in range(2):
+            multiply_z("bank4", 0, adj_mx, all_nodes)
+        normalise(1)
+        quantise_cf(0)
+        quantise_cf(1)
+        for c in (0, 1):
+            multiply_cf(c, 0, 2)
+        normalise(2)
+        normalise(3)
+        quantise_cf(2)
+        multiply_cf(2, 0, 2)
+        for c in range(LAST):
+            multiply_cf(c, 2, 1)
+        quantise_cf(LAST)
+        for c in range(LAST):
+            multiply_cf(c, LAST, 1)
+        multiply_cf(LAST, 0, CHUNKS)
+        for c in range(CHUNKS):
+            mask_and_sum(c)
+
         output = keep.tile([P, CHUNKS, FEAT], F32)
         nc.vector.scalar_tensor_tensor(
             out=output[:],
@@ -302,57 +365,16 @@ def tile_pmodel_pb_s_kernel(tc, adj1, hw, bg2, hm, Wm2, bm2, w_gl2, out_0, out_1
             op0=ALU.mult,
             op1=ALU.add,
         )
-        nc.sync.dma_start(out=out_0.rearrange("(p c) f -> p c f", c=CHUNKS), in_=output[:])
-
-        half_adj = keep.tile([P, CHUNKS, NODES], BF16)
-        for pair in range(PAIRS):
-            chunks = slice(2 * pair, 2 * pair + 2)
-            nc.scalar.mul(out=half_adj[:, chunks, :], in_=adj_sb[:, chunks, :], mul=0.5)
-
-        def multiply_cf(att, c, first, count):
-            nodes = slice(c * P, (c + 1) * P)
-            others = slice(first * P, (first + count) * P)
-            nc.tensor.matmul_mx(
-                out=att[:, others],
-                lhsT=cf_codes[:, nodes].bitcast(FP8X4),
-                lhsT_scale=cf_scales[:, nodes],
-                rhs=cf_codes[:, others].bitcast(FP8X4),
-                rhs_scale=cf_scales[:, others],
-                start=True,
-                stop=True,
-            )
-
-        att_banks = []
-        for c, tag in enumerate(("stage0", "stage1", "z1s", "z2s")):
-            att_banks.append(psum.tile([P, NODES], F32, tag=tag, name="att"))
-        for c in range(LAST):
-            multiply_cf(att_banks[c], c, 0, 2)
-            multiply_cf(att_banks[c], c, 2, 1)
-        for c in range(LAST):
-            multiply_cf(att_banks[c], c, LAST, 1)
-        multiply_cf(att_banks[LAST], LAST, 0, CHUNKS)
-
-        masked = keep.tile([P, CHUNKS, NODES], F32)
-        row_sum = keep.tile([P, CHUNKS], F32)
-        twice_sum = keep.tile([P, CHUNKS], F32)
-        half_inv_sum = keep.tile([P, CHUNKS], F32)
-        adj = keep.tile([P, CHUNKS, NODES], F32)
-        adj_rows = out_1.rearrange("(p c) m -> p c m", c=CHUNKS)
-
-        def mask_and_sum(c):
-            nc.scalar.activation(
-                out=masked[:, c, :].rearrange("n (j c) -> n j c", c=CHUNKS),
-                in_=att_banks[c][:].rearrange("n (c j) -> n j c", c=CHUNKS),
-                func=ACT.Relu,
-                scale=0.5,
-                accum_out=row_sum[:, c : c + 1],
-            )
+        nc.sync.dma_start(
+            out=out_0.rearrange("(h q j) f -> q h j f", h=PAIRS, j=2),
+            in_=output[:].rearrange("q (h j) f -> q h j f", h=PAIRS),
+        )
 
         def floor_sum(c):
             nc.vector.tensor_scalar(
                 out=twice_sum[:, c : c + 1],
                 in0=row_sum[:, c : c + 1],
-                scalar1=EPS,
+                scalar1=2 * EPS,
                 scalar2=2.0,
                 op0=ALU.max,
                 op1=ALU.mult,
@@ -361,7 +383,8 @@ def tile_pmodel_pb_s_kernel(tc, adj1, hw, bg2, hm, Wm2, bm2, w_gl2, out_0, out_1
         def invert_sum(c):
             nc.vector.reciprocal(out=half_inv_sum[:, c : c + 1], in_=twice_sum[:, c : c + 1])
 
-        def average(c, columns):
+        def average(c, pair):
+            columns = pair_nodes[pair]
             nc.vector.scalar_tensor_tensor(
                 out=adj[:, c, columns],
                 in0=masked[:, c, columns],
@@ -370,16 +393,14 @@ def tile_pmodel_pb_s_kernel(tc, adj1, hw, bg2, hm, Wm2, bm2, w_gl2, out_0, out_1
                 op0=ALU.mult,
                 op1=ALU.add,
             )
-            nc.sync.dma_start(out=adj_rows[:, c, columns], in_=adj[:, c, columns])
+            nc.sync.dma_start(out=adj_rows[c // 2][:, c % 2, columns], in_=adj[:, c, columns])
 
-        for c in range(CHUNKS):
-            mask_and_sum(c)
         floor_sum(0)
         invert_sum(0)
         for c in range(CHUNKS):
             if c + 1 < CHUNKS:
                 floor_sum(c + 1)
-            average(c, slice(0, NODES // 2))
+            average(c, 0)
             if c + 1 < CHUNKS:
                 invert_sum(c + 1)
-            average(c, slice(NODES // 2, NODES))
+            average(c, 1)

@@ -49,7 +49,7 @@ def tile_pmodel_pb_s_kernel(tc, adj1, hw, bg2, hm, Wm2, bm2, w_gl2, out_0, out_1
         table_warm = keep.tile([P, 1], F32)
         nc.scalar.activation(out=table_warm[:], in_=one[:], func=ACT.Abs_reciprocal_sqrt)
 
-        warm_bank = psum.tile([P, P], F32, tag="bank7")
+        warm_bank = psum.tile([P, P], F32, tag="bank6")
 
         def keep_warm(count):
             for i in range(count):
@@ -60,21 +60,26 @@ def tile_pmodel_pb_s_kernel(tc, adj1, hw, bg2, hm, Wm2, bm2, w_gl2, out_0, out_1
         make_identity(nc, ident_f32[:])
         make_identity(nc, ident_bf16[:])
 
-        def load_nodes(x_sb, x_dram):
-            x_rows = x_dram.rearrange("(h q j) k -> h q j k", h=PAIRS, j=2)
-            for pair in range(PAIRS):
-                nc.sync.dma_start(out=x_sb[:, 2 * pair : 2 * pair + 2, :], in_=x_rows[pair])
-
         adj_sb = keep.tile([P, CHUNKS, NODES], BF16)
         hm_sb = keep.tile([P, CHUNKS, NODES], BF16)
         weight_raw = keep.tile([P, PARTS, PACK, FEAT], BF16)
-        load_nodes(adj_sb, adj1)
-        for m, weight in enumerate((hw, Wm2)):
+
+        def load_pair(x_sb, x_dram, pair):
+            x_rows = x_dram.rearrange("(h q j) k -> h q j k", h=PAIRS, j=2)
+            nc.sync.dma_start(out=x_sb[:, 2 * pair : 2 * pair + 2, :], in_=x_rows[pair])
+
+        def load_weight(m, weight):
             nc.sync.dma_start(
                 out=weight_raw[:, m].rearrange("q (u e) f -> q u e f", u=2),
                 in_=weight.rearrange("(u q e) f -> q u e f", u=2, e=2),
             )
-        load_nodes(hm_sb, hm)
+
+        load_pair(adj_sb, adj1, 0)
+        load_weight(0, hw)
+        load_pair(hm_sb, hm, 0)
+        load_weight(1, Wm2)
+        load_pair(adj_sb, adj1, 1)
+        load_pair(hm_sb, hm, 1)
 
         def make_operand(name):
             return {
@@ -83,9 +88,9 @@ def tile_pmodel_pb_s_kernel(tc, adj1, hw, bg2, hm, Wm2, bm2, w_gl2, out_0, out_1
                 "scales": keep.tile([P, NODES], U8, align_bytes=64, name=name + "_scales"),
             }
 
-        def flip_chunk(x_sb, c):
+        def flip_chunk(x_sb, c, bank):
             words = x_sb[:].bitcast(F32)
-            flipped = psum.tile([P, 2, P], F32, tag="stage%d" % c, name="flipped")
+            flipped = psum.tile([P, 2, P], F32, tag="bank%d" % bank, name="flipped")
             for u in range(2):
                 nc.tensor.transpose(flipped[:, u, :], words[:, c, u * P : (u + 1) * P], ident_f32[:])
             return flipped
@@ -119,27 +124,35 @@ def tile_pmodel_pb_s_kernel(tc, adj1, hw, bg2, hm, Wm2, bm2, w_gl2, out_0, out_1
         scalar_copy = nc.scalar.copy
         adj_mx = make_operand("adj")
         hm_mx = make_operand("hm")
-        keep_warm(3)
-        for c, copy in enumerate((scalar_copy, vector_copy, vector_copy, vector_copy)):
-            group_chunk(adj_mx, c, flip_chunk(adj_sb, c), copy)
-        keep_warm(3)
-        group_weight(0)
-        group_weight(1)
-        quantise_pair(adj_mx, 0)
-        quantise_pair(adj_mx, 1)
-        quantise_weight(0)
-        hm_flipped = [flip_chunk(hm_sb, c) for c in (0, 1)]
+        def flip_and_group(x_sb, operand, c, bank, copy):
+            group_chunk(operand, c, flip_chunk(x_sb, c, bank), copy)
 
-        vector_bank = psum.tile([P, P], BF16, tag="bank5")
+        keep_warm(3)
+        for c in (0, 1):
+            flip_and_group(adj_sb, adj_mx, c, c, vector_copy)
+        keep_warm(1)
+        group_weight(0)
+        quantise_pair(adj_mx, 0)
+        flip_and_group(hm_sb, hm_mx, 0, 2, scalar_copy)
+        flip_and_group(hm_sb, hm_mx, 1, 3, vector_copy)
+        quantise_weight(0)
+        group_weight(1)
+
+        vector_bank = psum.tile([P, P], BF16, tag="bank4")
         nc.tensor.transpose(vector_bank[:], rows[:], ident_bf16[:])
-        bias_bank = psum.tile([P, FEAT], F32, tag="bank6")
+        bias_bank = psum.tile([P, FEAT], F32, tag="bank5")
         nc.tensor.matmul(out=bias_bank[:], lhsT=pick_bias[:], rhs=rows[:], start=True, stop=True)
-        hm_flipped += [flip_chunk(hm_sb, c) for c in (2, 3)]
+        keep_warm(1)
         vectors = keep.tile([P, PARTS + PERSP * PARTS], F32)
         weight_sq = keep.tile([P, PARTS, PERSP], F32)
-        weight_bias = keep.tile([P, PERSP], F32)
+        weight_bias = keep.tile([P, PARTS, PERSP], F32)
         half_bias = keep.tile([P, FEAT], F32)
         weight_columns = vectors[:, PARTS : PARTS + PERSP * PARTS].rearrange("f (p m) -> f m p", m=PARTS)
+        nc.vector.tensor_copy(out=vectors[:], in_=vector_bank[:, 0 : PARTS + PERSP * PARTS])
+        nc.scalar.activation(out=half_bias[:], in_=bias_bank[:], func=ACT.Copy, scale=0.5)
+        quantise_pair(hm_mx, 0)
+        quantise_weight(1)
+        nc.vector.tensor_tensor(out=weight_sq[:], in0=weight_columns, in1=weight_columns, op=ALU.mult)
 
         def bias_column(m):
             return vectors[:, m : m + 1]
@@ -148,20 +161,23 @@ def tile_pmodel_pb_s_kernel(tc, adj1, hw, bg2, hm, Wm2, bm2, w_gl2, out_0, out_1
             j = PARTS + PARTS * p + m
             return vectors[:, j : j + 1]
 
-        group_chunk(hm_mx, 0, hm_flipped[0], scalar_copy)
-        nc.scalar.activation(out=half_bias[:], in_=bias_bank[:], func=ACT.Copy, scale=0.5)
-        nc.vector.tensor_copy(out=vectors[:], in_=vector_bank[:, 0 : PARTS + PERSP * PARTS])
-        group_chunk(hm_mx, 1, hm_flipped[1], vector_copy)
-        quantise_weight(1)
-        quantise_pair(hm_mx, 0)
-        nc.vector.tensor_tensor(out=weight_sq[:], in0=weight_columns, in1=weight_columns, op=ALU.mult)
-        group_chunk(hm_mx, 2, hm_flipped[2], scalar_copy)
-        group_chunk(hm_mx, 3, hm_flipped[3], vector_copy)
-        nc.vector.tensor_scalar_mul(out=weight_bias[:], in0=weight_columns[:, 0, :], scalar1=bias_column(0))
-        quantise_pair(hm_mx, 1)
+        adj_flipped = [flip_chunk(adj_sb, c, c - 2) for c in (2, 3)]
+        group_chunk(adj_mx, 2, adj_flipped[0], vector_copy)
+        nc.vector.tensor_tensor(
+            out=weight_bias[:],
+            in0=weight_columns,
+            in1=vectors[:, 0:PARTS].unsqueeze(2).to_broadcast([P, PARTS, PERSP]),
+            op=ALU.mult,
+        )
+        group_chunk(adj_mx, 3, adj_flipped[1], vector_copy)
+        keep_warm(1)
 
-        def multiply_z(tag, m, operand, nodes):
-            bank = psum.tile([P, nodes.stop - nodes.start], F32, tag=tag, name="z")
+        pair_nodes = [slice(pair * HALF, (pair + 1) * HALF) for pair in range(PAIRS)]
+
+        def multiply_z(tag, m, pair):
+            nodes = pair_nodes[pair]
+            operand = (adj_mx, hm_mx)[m]
+            bank = psum.tile([P, HALF], F32, tag=tag, name="z")
             nc.tensor.matmul_mx(
                 out=bank[:],
                 lhsT=weight_codes[:, m, :].bitcast(FP8X4),
@@ -177,32 +193,36 @@ def tile_pmodel_pb_s_kernel(tc, adj1, hw, bg2, hm, Wm2, bm2, w_gl2, out_0, out_1
         weighted = keep.tile([P, PERSP, PARTS, NODES], F32)
         norm_floor = keep.tile([P, CHUNKS, PERSP], F32)
         inv_norm = keep.tile([P, CHUNKS, PERSP], F32)
-        all_nodes = slice(0, NODES)
-        pair_nodes = [slice(pair * HALF, (pair + 1) * HALF) for pair in range(PAIRS)]
 
-        def square(m, z, nodes):
-            nc.scalar.activation(out=squares[:, m, nodes], in_=z[:], func=ACT.Square, bias=bias_column(m))
-
-        def weigh_z1(p):
+        def square(m, pair, z):
             nc.scalar.activation(
-                out=weighted[:, p, 0, :],
-                in_=z1[:],
-                func=ACT.Identity,
-                scale=weight_column(p, 0),
-                bias=weight_bias[:, p : p + 1],
+                out=squares[:, m, pair_nodes[pair]], in_=z[:], func=ACT.Square, bias=bias_column(m)
             )
 
-        def weigh_z2(p, pair):
+        def weigh_on_scalar(p, m, pair, z):
+            nc.scalar.activation(
+                out=weighted[:, p, m, pair_nodes[pair]],
+                in_=z[:],
+                func=ACT.Identity,
+                scale=weight_column(p, m),
+                bias=weight_bias[:, m, p : p + 1],
+            )
+
+        def weigh_on_vector(p, m, pair, z):
             nc.vector.tensor_scalar(
-                out=weighted[:, p, 1, pair_nodes[pair]],
-                in0=z2_v[pair][:],
-                scalar1=bias_column(1),
-                scalar2=weight_column(p, 1),
+                out=weighted[:, p, m, pair_nodes[pair]],
+                in0=z[:],
+                scalar1=bias_column(m),
+                scalar2=weight_column(p, m),
                 op0=ALU.add,
                 op1=ALU.mult,
             )
 
+        norm_banks = []
+
         def sum_squares(m, pair):
+            if m == 0:
+                norm_banks.append(psum.tile([P, 2, PERSP], F32, tag="bank%d" % pair, name="norm_bank"))
             for j in range(2):
                 c = 2 * pair + j
                 nc.tensor.matmul(
@@ -213,9 +233,13 @@ def tile_pmodel_pb_s_kernel(tc, adj1, hw, bg2, hm, Wm2, bm2, w_gl2, out_0, out_1
                     stop=(m == PARTS - 1 and j == 1),
                 )
 
+        def floor_norms(pair):
+            nc.vector.tensor_scalar_max(
+                out=norm_floor[:, 2 * pair : 2 * pair + 2, :], in0=norm_banks[pair][:], scalar1=EPS * EPS
+            )
+
         def invert_norms(pair):
             chunks = slice(2 * pair, 2 * pair + 2)
-            nc.vector.tensor_scalar_max(out=norm_floor[:, chunks, :], in0=norm_banks[pair][:], scalar1=EPS * EPS)
             nc.scalar.activation(
                 out=inv_norm[:, chunks, :], in_=norm_floor[:, chunks, :], func=ACT.Abs_reciprocal_sqrt
             )
@@ -228,34 +252,43 @@ def tile_pmodel_pb_s_kernel(tc, adj1, hw, bg2, hm, Wm2, bm2, w_gl2, out_0, out_1
                 nc.tensor.transpose(bank[:, p, :], inv_norm[:, c, p : p + 1].to_broadcast([P, P]), ident_f32[:])
             spread_banks.append(bank)
 
-        z1 = multiply_z("bank4", 0, adj_mx, all_nodes)
-        square(0, z1, all_nodes)
-        for i in range(2):
-            multiply_z("bank5", 0, adj_mx, all_nodes)
-        z2_s = [multiply_z("bank6", 1, hm_mx, pair_nodes[0])]
-        z2_v = [multiply_z("bank7", 1, hm_mx, pair_nodes[0])]
-        square(1, z2_s[0], pair_nodes[0])
-        norm_banks = [
-            psum.tile([P, 2, PERSP], F32, tag="stage%d" % pair, name="norm_bank") for pair in range(PAIRS)
-        ]
+        z1_first = multiply_z("bank4", 0, 0)
+        square(0, 0, z1_first)
+        hm_flipped = [flip_chunk(hm_sb, c, c) for c in (2, 3)]
+        group_chunk(hm_mx, 2, hm_flipped[0], scalar_copy)
+        group_chunk(hm_mx, 3, hm_flipped[1], vector_copy)
+        z2_first = multiply_z("bank5", 1, 0)
+        z2_vector = multiply_z("bank6", 1, 0)
+        quantise_pair(adj_mx, 1)
+        quantise_pair(hm_mx, 1)
+        square(1, 0, z2_first)
+        multiply_z("bank7", 0, 0)
         sum_squares(0, 0)
         sum_squares(1, 0)
-        z2_s.append(multiply_z("stage2", 1, hm_mx, pair_nodes[1]))
-        z2_v.append(multiply_z("stage3", 1, hm_mx, pair_nodes[1]))
         for p in range(PERSP):
-            weigh_z1(p)
-        for p in range(PERSP):
-            weigh_z2(p, 0)
-        sum_squares(0, 1)
-
+            weigh_on_scalar(p, 0, 0, z1_first)
+        weigh_on_vector(0, 1, 0, z2_vector)
+        floor_norms(0)
+        weigh_on_vector(1, 1, 0, z2_vector)
+        z1_second = multiply_z("bank7", 0, 1)
+        z2_second = multiply_z("bank2", 1, 1)
         invert_norms(0)
-        for c in (0, 1):
-            spread_norms(c, ("bank5", "bank7")[c])
-        square(1, z2_s[1], pair_nodes[1])
+        multiply_z("bank5", 0, 0)
+        multiply_z("bank1", 0, 0)
+        square(0, 1, z1_second)
+        for c, tag in ((0, "bank3"), (1, "bank6")):
+            spread_norms(c, tag)
+        square(1, 1, z2_second)
+        sum_squares(0, 1)
         sum_squares(1, 1)
+        for p in range(PERSP):
+            weigh_on_scalar(p, 0, 1, z1_second)
+        for p in range(PERSP):
+            weigh_on_scalar(p, 1, 1, z2_second)
 
-        sum_bank = psum.tile([P, CHUNKS, FEAT], F32, tag="bank6")
-        for c in range(CHUNKS):
+        sum_bank = psum.tile([P, CHUNKS, FEAT], F32, tag="bank4")
+
+        def multiply_sum(c):
             nodes = slice(c * P, (c + 1) * P)
             for m, operand in enumerate((adj_mx, hm_mx)):
                 nc.tensor.matmul_mx(
@@ -268,15 +301,13 @@ def tile_pmodel_pb_s_kernel(tc, adj1, hw, bg2, hm, Wm2, bm2, w_gl2, out_0, out_1
                     stop=(m == PARTS - 1),
                 )
 
+        for c in (0, 1):
+            multiply_sum(c)
+
         half_adj = keep.tile([P, CHUNKS, NODES], BF16)
 
         def halve_adj(c):
             nc.scalar.mul(out=half_adj[:, c, :], in_=adj_sb[:, c, :], mul=0.5)
-
-        halve_adj(0)
-        halve_adj(1)
-        for p in range(PERSP):
-            weigh_z2(p, 1)
 
         cf_grouped = keep.tile([P, CHUNKS, P, PACK], BF16, align_bytes=64)
         cf_codes = keep.tile([P, NODES], U32, align_bytes=64)
@@ -299,7 +330,7 @@ def tile_pmodel_pb_s_kernel(tc, adj1, hw, bg2, hm, Wm2, bm2, w_gl2, out_0, out_1
             )
 
         att_banks = [
-            psum.tile([P, NODES], F32, tag=tag, name="att") for tag in ("bank4", "stage1", "stage2", "bank5")
+            psum.tile([P, NODES], F32, tag=tag, name="att") for tag in ("bank7", "bank2", "bank1", "bank3")
         ]
 
         def multiply_cf(c, first, count):
@@ -331,28 +362,27 @@ def tile_pmodel_pb_s_kernel(tc, adj1, hw, bg2, hm, Wm2, bm2, w_gl2, out_0, out_1
             )
 
         normalise(0)
-        invert_norms(1)
-        halve_adj(2)
-        halve_adj(3)
-        for c in (2, 3):
-            spread_norms(c, ("stage0", "stage3")[c - 2])
-        for i in range(2):
-            multiply_z("bank4", 0, adj_mx, all_nodes)
-        normalise(1)
         quantise_cf(0)
+        floor_norms(1)
+        invert_norms(1)
+        for c in range(CHUNKS):
+            halve_adj(c)
+        for c, tag in ((2, "bank5"), (3, "bank0")):
+            spread_norms(c, tag)
+        for c in (2, 3):
+            multiply_sum(c)
+        normalise(1)
         quantise_cf(1)
         for c in (0, 1):
             multiply_cf(c, 0, 2)
         normalise(2)
         normalise(3)
         quantise_cf(2)
-        multiply_cf(2, 0, 2)
-        for c in range(LAST):
-            multiply_cf(c, 2, 1)
-        quantise_cf(LAST)
-        for c in range(LAST):
-            multiply_cf(c, LAST, 1)
-        multiply_cf(LAST, 0, CHUNKS)
+        quantise_cf(3)
+        for c in (0, 1):
+            multiply_cf(c, 2, 2)
+        for c in (2, 3):
+            multiply_cf(c, 0, CHUNKS)
         for c in range(CHUNKS):
             mask_and_sum(c)
 

@@ -42,9 +42,6 @@ def tile_pmodel_pb_s_kernel(tc, adj1, hw, bg2, hm, Wm2, bm2, w_gl2, out_0, out_1
         nc.vector.memset(one[:], 1.0)
         nc.vector.memset(pick_bias[:], 0.0)
         nc.vector.memset(pick_bias[0:2, :], 1.0)
-        nc.scalar.dma_start(out=rows[2:6, :], in_=w_gl2.rearrange("p (m f) -> (p m) f", m=PARTS))
-        nc.scalar.dma_start(out=rows[0:1, :], in_=bg2.rearrange("(o f) -> o f", o=1))
-        nc.scalar.dma_start(out=rows[1:2, :], in_=bm2.rearrange("(o f) -> o f", o=1))
 
         table_warm = keep.tile([P, 1], F32)
         nc.scalar.activation(out=table_warm[:], in_=one[:], func=ACT.Abs_reciprocal_sqrt)
@@ -77,6 +74,9 @@ def tile_pmodel_pb_s_kernel(tc, adj1, hw, bg2, hm, Wm2, bm2, w_gl2, out_0, out_1
         load_pair(adj_sb, adj1, 0)
         load_weight(0, hw)
         load_pair(hm_sb, hm, 0)
+        nc.sync.dma_start(out=rows[2:6, :], in_=w_gl2.rearrange("p (m f) -> (p m) f", m=PARTS))
+        nc.sync.dma_start(out=rows[0:1, :], in_=bg2.rearrange("(o f) -> o f", o=1))
+        nc.sync.dma_start(out=rows[1:2, :], in_=bm2.rearrange("(o f) -> o f", o=1))
         load_weight(1, Wm2)
         load_pair(adj_sb, adj1, 1)
         load_pair(hm_sb, hm, 1)
@@ -140,7 +140,7 @@ def tile_pmodel_pb_s_kernel(tc, adj1, hw, bg2, hm, Wm2, bm2, w_gl2, out_0, out_1
 
         vector_bank = psum.tile([P, P], BF16, tag="bank4")
         nc.tensor.transpose(vector_bank[:], rows[:], ident_bf16[:])
-        bias_bank = psum.tile([P, FEAT], F32, tag="bank5")
+        bias_bank = psum.tile([P, FEAT], F32, tag="bank7")
         nc.tensor.matmul(out=bias_bank[:], lhsT=pick_bias[:], rhs=rows[:], start=True, stop=True)
         keep_warm(1)
         vectors = keep.tile([P, PARTS + PERSP * PARTS], F32)
@@ -149,7 +149,6 @@ def tile_pmodel_pb_s_kernel(tc, adj1, hw, bg2, hm, Wm2, bm2, w_gl2, out_0, out_1
         half_bias = keep.tile([P, FEAT], F32)
         weight_columns = vectors[:, PARTS : PARTS + PERSP * PARTS].rearrange("f (p m) -> f m p", m=PARTS)
         nc.vector.tensor_copy(out=vectors[:], in_=vector_bank[:, 0 : PARTS + PERSP * PARTS])
-        nc.scalar.activation(out=half_bias[:], in_=bias_bank[:], func=ACT.Copy, scale=0.5)
         quantise_pair(hm_mx, 0)
         quantise_weight(1)
         nc.vector.tensor_tensor(out=weight_sq[:], in0=weight_columns, in1=weight_columns, op=ALU.mult)
@@ -162,7 +161,8 @@ def tile_pmodel_pb_s_kernel(tc, adj1, hw, bg2, hm, Wm2, bm2, w_gl2, out_0, out_1
             return vectors[:, j : j + 1]
 
         adj_flipped = [flip_chunk(adj_sb, c, c - 2) for c in (2, 3)]
-        group_chunk(adj_mx, 2, adj_flipped[0], vector_copy)
+        group_chunk(adj_mx, 2, adj_flipped[0], scalar_copy)
+        nc.scalar.activation(out=half_bias[:], in_=bias_bank[:], func=ACT.Copy, scale=0.5)
         nc.vector.tensor_tensor(
             out=weight_bias[:],
             in0=weight_columns,
@@ -174,10 +174,9 @@ def tile_pmodel_pb_s_kernel(tc, adj1, hw, bg2, hm, Wm2, bm2, w_gl2, out_0, out_1
 
         pair_nodes = [slice(pair * HALF, (pair + 1) * HALF) for pair in range(PAIRS)]
 
-        def multiply_z(tag, m, pair):
-            nodes = pair_nodes[pair]
+        def multiply_z(tag, m, nodes):
             operand = (adj_mx, hm_mx)[m]
-            bank = psum.tile([P, HALF], F32, tag=tag, name="z")
+            bank = psum.tile([P, nodes.stop - nodes.start], F32, tag=tag, name="z")
             nc.tensor.matmul_mx(
                 out=bank[:],
                 lhsT=weight_codes[:, m, :].bitcast(FP8X4),
@@ -188,6 +187,9 @@ def tile_pmodel_pb_s_kernel(tc, adj1, hw, bg2, hm, Wm2, bm2, w_gl2, out_0, out_1
                 stop=True,
             )
             return bank
+
+        def keep_warm_mx(tag, nodes):
+            multiply_z(tag, 0, nodes)
 
         squares = keep.tile([P, PARTS, NODES], F32)
         weighted = keep.tile([P, PERSP, PARTS, NODES], F32)
@@ -252,17 +254,17 @@ def tile_pmodel_pb_s_kernel(tc, adj1, hw, bg2, hm, Wm2, bm2, w_gl2, out_0, out_1
                 nc.tensor.transpose(bank[:, p, :], inv_norm[:, c, p : p + 1].to_broadcast([P, P]), ident_f32[:])
             spread_banks.append(bank)
 
-        z1_first = multiply_z("bank4", 0, 0)
+        z1_first = multiply_z("bank4", 0, pair_nodes[0])
         square(0, 0, z1_first)
         hm_flipped = [flip_chunk(hm_sb, c, c) for c in (2, 3)]
         group_chunk(hm_mx, 2, hm_flipped[0], scalar_copy)
         group_chunk(hm_mx, 3, hm_flipped[1], vector_copy)
-        z2_first = multiply_z("bank5", 1, 0)
-        z2_vector = multiply_z("bank6", 1, 0)
+        z2_first = multiply_z("bank5", 1, pair_nodes[0])
+        z2_vector = multiply_z("bank6", 1, pair_nodes[0])
+        keep_warm_mx("bank7", pair_nodes[0])
         quantise_pair(adj_mx, 1)
         quantise_pair(hm_mx, 1)
         square(1, 0, z2_first)
-        multiply_z("bank7", 0, 0)
         sum_squares(0, 0)
         sum_squares(1, 0)
         for p in range(PERSP):
@@ -270,17 +272,17 @@ def tile_pmodel_pb_s_kernel(tc, adj1, hw, bg2, hm, Wm2, bm2, w_gl2, out_0, out_1
         weigh_on_vector(0, 1, 0, z2_vector)
         floor_norms(0)
         weigh_on_vector(1, 1, 0, z2_vector)
-        z1_second = multiply_z("bank7", 0, 1)
-        z2_second = multiply_z("bank2", 1, 1)
-        invert_norms(0)
-        multiply_z("bank5", 0, 0)
-        multiply_z("bank1", 0, 0)
+        z1_second = multiply_z("bank7", 0, pair_nodes[1])
+        z2_second = multiply_z("bank2", 1, pair_nodes[1])
         square(0, 1, z1_second)
-        for c, tag in ((0, "bank3"), (1, "bank6")):
-            spread_norms(c, tag)
+        invert_norms(0)
+        for tag in ("bank5", "bank1"):
+            keep_warm_mx(tag, slice(0, NODES))
+        spread_norms(0, "bank3")
         square(1, 1, z2_second)
         sum_squares(0, 1)
         sum_squares(1, 1)
+        spread_norms(1, "bank6")
         for p in range(PERSP):
             weigh_on_scalar(p, 0, 1, z1_second)
         for p in range(PERSP):
@@ -301,7 +303,7 @@ def tile_pmodel_pb_s_kernel(tc, adj1, hw, bg2, hm, Wm2, bm2, w_gl2, out_0, out_1
                     stop=(m == PARTS - 1),
                 )
 
-        for c in (0, 1):
+        for c in range(CHUNKS):
             multiply_sum(c)
 
         half_adj = keep.tile([P, CHUNKS, NODES], BF16)
@@ -362,23 +364,25 @@ def tile_pmodel_pb_s_kernel(tc, adj1, hw, bg2, hm, Wm2, bm2, w_gl2, out_0, out_1
             )
 
         normalise(0)
-        quantise_cf(0)
         floor_norms(1)
         invert_norms(1)
         for c in range(CHUNKS):
             halve_adj(c)
         for c, tag in ((2, "bank5"), (3, "bank0")):
             spread_norms(c, tag)
-        for c in (2, 3):
-            multiply_sum(c)
         normalise(1)
+        quantise_cf(0)
         quantise_cf(1)
+        for tag in ("bank6", "bank1"):
+            keep_warm_mx(tag, slice(0, NODES))
         for c in (0, 1):
             multiply_cf(c, 0, 2)
         normalise(2)
         normalise(3)
         quantise_cf(2)
         quantise_cf(3)
+        for tag in ("bank6", "bank3"):
+            keep_warm_mx(tag, slice(0, NODES))
         for c in (0, 1):
             multiply_cf(c, 2, 2)
         for c in (2, 3):

@@ -172,6 +172,7 @@ def tile_pmodel_pb_s_kernel(tc, adj1, hw, bg2, hm, Wm2, bm2, w_gl2, out_0, out_1
         group_chunk(adj_mx, 3, adj_flipped[1], vector_copy)
         keep_warm(1)
 
+        all_nodes = slice(0, NODES)
         pair_nodes = [slice(pair * HALF, (pair + 1) * HALF) for pair in range(PAIRS)]
 
         def multiply_z(tag, m, nodes):
@@ -266,23 +267,22 @@ def tile_pmodel_pb_s_kernel(tc, adj1, hw, bg2, hm, Wm2, bm2, w_gl2, out_0, out_1
         quantise_pair(hm_mx, 1)
         square(1, 0, z2_first)
         sum_squares(0, 0)
+        z1_second = multiply_z("bank7", 0, pair_nodes[1])
         sum_squares(1, 0)
         for p in range(PERSP):
             weigh_on_scalar(p, 0, 0, z1_first)
         weigh_on_vector(0, 1, 0, z2_vector)
         floor_norms(0)
         weigh_on_vector(1, 1, 0, z2_vector)
-        z1_second = multiply_z("bank7", 0, pair_nodes[1])
         z2_second = multiply_z("bank2", 1, pair_nodes[1])
         square(0, 1, z1_second)
         invert_norms(0)
-        for tag in ("bank5", "bank1"):
-            keep_warm_mx(tag, slice(0, NODES))
+        keep_warm_mx("bank5", all_nodes)
+        sum_squares(0, 1)
         spread_norms(0, "bank3")
         square(1, 1, z2_second)
-        sum_squares(0, 1)
-        sum_squares(1, 1)
         spread_norms(1, "bank6")
+        sum_squares(1, 1)
         for p in range(PERSP):
             weigh_on_scalar(p, 0, 1, z1_second)
         for p in range(PERSP):
@@ -305,6 +305,7 @@ def tile_pmodel_pb_s_kernel(tc, adj1, hw, bg2, hm, Wm2, bm2, w_gl2, out_0, out_1
 
         for c in range(CHUNKS):
             multiply_sum(c)
+        keep_warm_mx("bank3", all_nodes)
 
         half_adj = keep.tile([P, CHUNKS, NODES], BF16)
 
@@ -374,15 +375,15 @@ def tile_pmodel_pb_s_kernel(tc, adj1, hw, bg2, hm, Wm2, bm2, w_gl2, out_0, out_1
         quantise_cf(0)
         quantise_cf(1)
         for tag in ("bank6", "bank1"):
-            keep_warm_mx(tag, slice(0, NODES))
+            keep_warm_mx(tag, all_nodes)
         for c in (0, 1):
             multiply_cf(c, 0, 2)
         normalise(2)
         normalise(3)
         quantise_cf(2)
         quantise_cf(3)
-        for tag in ("bank6", "bank3"):
-            keep_warm_mx(tag, slice(0, NODES))
+        for tag in ("bank6", "bank5"):
+            keep_warm_mx(tag, all_nodes)
         for c in (0, 1):
             multiply_cf(c, 2, 2)
         for c in (2, 3):

@@ -332,34 +332,41 @@ def tile_pmodel_pb_s_kernel(tc, adj1, hw, bg2, hm, Wm2, bm2, w_gl2, out_0, out_1
                 in_=cf_grouped[:, c].rearrange("q n t -> q (n t)"),
             )
 
-        att_banks = [
-            psum.tile([P, NODES], F32, tag=tag, name="att") for tag in ("bank7", "bank2", "bank1", "bank3")
-        ]
-
-        def multiply_cf(c, first, count):
+        def multiply_cf(out, c, columns):
             nodes = slice(c * P, (c + 1) * P)
-            others = slice(first * P, (first + count) * P)
             nc.tensor.matmul_mx(
-                out=att_banks[c][:, others],
+                out=out,
                 lhsT=cf_codes[:, nodes].bitcast(FP8X4),
                 lhsT_scale=cf_scales[:, nodes],
-                rhs=cf_codes[:, others].bitcast(FP8X4),
-                rhs_scale=cf_scales[:, others],
+                rhs=cf_codes[:, columns].bitcast(FP8X4),
+                rhs_scale=cf_scales[:, columns],
                 start=True,
                 stop=True,
             )
 
         masked = keep.tile([P, CHUNKS, NODES], F32)
+        half_sum = keep.tile([P, PAIRS, 2], F32)
+        first_twice = keep.tile([P, 2], F32)
         row_sum = keep.tile([P, CHUNKS], F32)
         twice_sum = keep.tile([P, CHUNKS], F32)
         half_inv_sum = keep.tile([P, CHUNKS], F32)
+        quarter_inv_sum = keep.tile([P, 2], F32)
         adj = keep.tile([P, CHUNKS, NODES], F32)
         adj_rows = out_1.rearrange("(h q j) m -> h q j m", h=PAIRS, j=2)
+
+        def mask_half(c, pair):
+            nc.scalar.activation(
+                out=masked[:, c, pair_nodes[pair]].rearrange("n (q j) -> n q j", j=2),
+                in_=att_halves[pair][c][:].rearrange("n (j q) -> n q j", j=2),
+                func=ACT.Relu,
+                scale=1.0 + pair,
+                accum_out=half_sum[:, pair, c : c + 1],
+            )
 
         def mask_and_sum(c):
             nc.scalar.activation(
                 out=masked[:, c, :].rearrange("n (h q j) -> n h q j", h=PAIRS, j=2),
-                in_=att_banks[c][:].rearrange("n (h j q) -> n h q j", h=PAIRS, j=2),
+                in_=att_rows[c][:].rearrange("n (h j q) -> n h q j", h=PAIRS, j=2),
                 func=ACT.Relu,
                 accum_out=row_sum[:, c : c + 1],
             )
@@ -376,19 +383,27 @@ def tile_pmodel_pb_s_kernel(tc, adj1, hw, bg2, hm, Wm2, bm2, w_gl2, out_0, out_1
         quantise_cf(1)
         for tag in ("bank6", "bank1"):
             keep_warm_mx(tag, all_nodes)
+        att_halves = [
+            [psum.tile([P, HALF], F32, tag=tag, name="att_half") for tag in tags]
+            for tags in (("bank7", "bank2"), ("bank0", "bank6"))
+        ]
         for c in (0, 1):
-            multiply_cf(c, 0, 2)
+            multiply_cf(att_halves[0][c][:], c, pair_nodes[0])
+            mask_half(c, 0)
         normalise(2)
         normalise(3)
         quantise_cf(2)
         quantise_cf(3)
-        for tag in ("bank6", "bank5"):
+        for tag in ("bank3", "bank5"):
             keep_warm_mx(tag, all_nodes)
+        att_rows = {c: psum.tile([P, NODES], F32, tag=tag, name="att_row") for c, tag in ((2, "bank1"), (3, "bank3"))}
         for c in (0, 1):
-            multiply_cf(c, 2, 2)
+            multiply_cf(att_halves[1][c][:], c, pair_nodes[1])
         for c in (2, 3):
-            multiply_cf(c, 0, CHUNKS)
-        for c in range(CHUNKS):
+            multiply_cf(att_rows[c][:], c, all_nodes)
+        for c in (0, 1):
+            mask_half(c, 1)
+        for c in (2, 3):
             mask_and_sum(c)
 
         output = keep.tile([P, CHUNKS, FEAT], F32)
@@ -418,24 +433,52 @@ def tile_pmodel_pb_s_kernel(tc, adj1, hw, bg2, hm, Wm2, bm2, w_gl2, out_0, out_1
         def invert_sum(c):
             nc.vector.reciprocal(out=half_inv_sum[:, c : c + 1], in_=twice_sum[:, c : c + 1])
 
-        def average(c, pair):
-            columns = pair_nodes[pair]
+        def average(c, columns, factor):
             nc.vector.scalar_tensor_tensor(
                 out=adj[:, c, columns],
                 in0=masked[:, c, columns],
-                scalar=half_inv_sum[:, c : c + 1],
+                scalar=factor,
                 in1=half_adj[:, c, columns],
                 op0=ALU.mult,
                 op1=ALU.add,
             )
             nc.sync.dma_start(out=adj_rows[c // 2][:, c % 2, columns], in_=adj[:, c, columns])
 
-        floor_sum(0)
+        def join_sums(c):
+            nc.vector.tensor_scalar(
+                out=twice_sum[:, c : c + 1],
+                in0=half_sum[:, 1, c : c + 1],
+                scalar1=first_twice[:, c : c + 1],
+                scalar2=4 * EPS,
+                op0=ALU.add,
+                op1=ALU.max,
+            )
+
+        def halve_factor(c):
+            nc.vector.tensor_scalar_mul(
+                out=quarter_inv_sum[:, c : c + 1], in0=half_inv_sum[:, c : c + 1], scalar1=0.5
+            )
+
+        def average_half(c, pair):
+            factor = quarter_inv_sum if (c < 2 and pair == 1) else half_inv_sum
+            average(c, pair_nodes[pair], factor[:, c : c + 1])
+
+        nc.vector.tensor_scalar_mul(out=first_twice[:], in0=half_sum[:, 0, :], scalar1=2.0)
+        join_sums(0)
         invert_sum(0)
-        for c in range(CHUNKS):
-            if c + 1 < CHUNKS:
-                floor_sum(c + 1)
-            average(c, 0)
-            if c + 1 < CHUNKS:
-                invert_sum(c + 1)
-            average(c, 1)
+        join_sums(1)
+        halve_factor(0)
+        average_half(0, 0)
+        invert_sum(1)
+        average_half(0, 1)
+        halve_factor(1)
+        floor_sum(2)
+        average_half(1, 0)
+        invert_sum(2)
+        average_half(1, 1)
+        floor_sum(3)
+        average_half(2, 0)
+        invert_sum(3)
+        average_half(2, 1)
+        average_half(3, 0)
+        average_half(3, 1)

from contextlib import ExitStack

import concourse.mybir as mybir
from concourse.masks import make_identity

F32 = mybir.dt.float32
BF16 = mybir.dt.bfloat16
U32 = mybir.dt.uint32
U8 = mybir.dt.uint8
FP8X4 = mybir.dt.float8_e4m3fn_x4
ACT = mybir.ActivationFunctionType
ALU = mybir.AluOpType

P = 128
PACK = 4
NODES = 512
CHUNKS = NODES // P
PAIRS = CHUNKS // 2
HALF = NODES // 2
LAST = CHUNKS - 1
FEAT = 128
PARTS = 2
PERSP = 2
EPS = 1e-12

FLOPS = 2 * NODES * NODES * FEAT * 2 + 2 * NODES * NODES * PERSP * PARTS * FEAT


def tile_pmodel_pb_s_kernel(tc, adj1, hw, bg2, hm, Wm2, bm2, w_gl2, out_0, out_1):
    nc = tc.nc
    with ExitStack() as ctx:
        keep = ctx.enter_context(tc.tile_pool(name="keep", bufs=1))
        psum = ctx.enter_context(tc.psum_pool(name="psum", bufs=1))
        ctx.enter_context(tc.manual_schedule())

        warm_in = keep.tile([P, P], F32)
        rows = keep.tile([P, FEAT], BF16)
        pick_bias = keep.tile([P, P], BF16)
        one = keep.tile([P, 1], F32)
        nc.vector.memset(rows[:], 0.0)
        nc.vector.memset(warm_in[:], 1.0)
        nc.vector.memset(one[:], 1.0)
        nc.vector.memset(pick_bias[:], 0.0)
        nc.vector.memset(pick_bias[0:2, :], 1.0)

        table_warm = keep.tile([P, 1], F32)
        nc.scalar.activation(out=table_warm[:], in_=one[:], func=ACT.Abs_reciprocal_sqrt)

        warm_bank = psum.tile([P, P], F32, tag="bank6")

        def keep_warm(count):
            for i in range(count):
                nc.tensor.matmul(out=warm_bank[:], lhsT=warm_in[:], rhs=warm_in[:], start=True, stop=True)

        ident_f32 = keep.tile([P, P], F32)
        ident_bf16 = keep.tile([P, P], BF16)
        make_identity(nc, ident_f32[:])
        make_identity(nc, ident_bf16[:])

        adj_sb = keep.tile([P, CHUNKS, NODES], BF16)
        hm_sb = keep.tile([P, CHUNKS, NODES], BF16)
        weight_raw = keep.tile([P, PARTS, PACK, FEAT], BF16)

        def load_pair(x_sb, x_dram, pair):
            x_rows = x_dram.rearrange("(h q j) k -> h q j k", h=PAIRS, j=2)
            nc.sync.dma_start(out=x_sb[:, 2 * pair : 2 * pair + 2, :], in_=x_rows[pair])

        def load_weight(m, weight):
            nc.sync.dma_start(
                out=weight_raw[:, m].rearrange("q (u e) f -> q u e f", u=2),
                in_=weight.rearrange("(u q e) f -> q u e f", u=2, e=2),
            )

        load_pair(adj_sb, adj1, 0)
        load_weight(0, hw)
        load_pair(hm_sb, hm, 0)
        nc.sync.dma_start(out=rows[2:6, :], in_=w_gl2.rearrange("p (m f) -> (p m) f", m=PARTS))
        nc.sync.dma_start(out=rows[0:1, :], in_=bg2.rearrange("(o f) -> o f", o=1))
        nc.sync.dma_start(out=rows[1:2, :], in_=bm2.rearrange("(o f) -> o f", o=1))
        load_weight(1, Wm2)
        load_pair(adj_sb, adj1, 1)
        load_pair(hm_sb, hm, 1)

        def make_operand(name):
            return {
                "grouped": keep.tile([P, CHUNKS, P, PACK], BF16, align_bytes=64, name=name + "_grouped"),
                "codes": keep.tile([P, NODES], U32, align_bytes=64, name=name + "_codes"),
                "scales": keep.tile([P, NODES], U8, align_bytes=64, name=name + "_scales"),
            }

        def flip_chunk(x_sb, c, bank):
            words = x_sb[:].bitcast(F32)
            flipped = psum.tile([P, 2, P], F32, tag="bank%d" % bank, name="flipped")
            for u in range(2):
                nc.tensor.transpose(flipped[:, u, :], words[:, c, u * P : (u + 1) * P], ident_f32[:])
            return flipped

        def group_chunk(operand, c, flipped, copy):
            copy(out=operand["grouped"][:].bitcast(F32)[:, c], in_=flipped[:].rearrange("q u n -> q n u"))

        def quantise_pair(operand, pair):
            nodes = slice(pair * HALF, (pair + 1) * HALF)
            nc.vector.quantize_mx(
                out=operand["codes"][:, nodes].bitcast(FP8X4),
                scales=operand["scales"][:, nodes],
                in_=operand["grouped"][:, 2 * pair : 2 * pair + 2].rearrange("q c n t -> q (c n t)"),
            )

        weight_grouped = keep.tile([P, PARTS, FEAT, PACK], BF16, align_bytes=64)
        weight_codes = keep.tile([P, PARTS, FEAT], U32, align_bytes=64)
        weight_scales = keep.tile([P, PARTS, FEAT], U8, align_bytes=64)

        def group_weight(m):
            nc.scalar.copy(out=weight_grouped[:, m], in_=weight_raw[:, m].rearrange("q t f -> q f t"))

        def quantise_weight(m):
            nc.vector.quantize_mx(
                out=weight_codes[:, m].bitcast(FP8X4),
                scales=weight_scales[:, m],
                in_=weight_grouped[:, m].rearrange("q f t -> q (f t)"),
            )

        vector_copy = nc.vector.tensor_copy
        scalar_copy = nc.scalar.copy
        adj_mx = make_operand("adj")
        hm_mx = make_operand("hm")
        def flip_and_group(x_sb, operand, c, bank, copy):
            group_chunk(operand, c, flip_chunk(x_sb, c, bank), copy)

        keep_warm(3)
        for c in (0, 1):
            flip_and_group(adj_sb, adj_mx, c, c, vector_copy)
        keep_warm(1)
        group_weight(0)
        quantise_pair(adj_mx, 0)
        flip_and_group(hm_sb, hm_mx, 0, 2, scalar_copy)
        flip_and_group(hm_sb, hm_mx, 1, 3, vector_copy)
        quantise_weight(0)
        group_weight(1)

        vector_bank = psum.tile([P, P], BF16, tag="bank4")
        nc.tensor.transpose(vector_bank[:], rows[:], ident_bf16[:])
        bias_bank = psum.tile([P, FEAT], F32, tag="bank7")
        nc.tensor.matmul(out=bias_bank[:], lhsT=pick_bias[:], rhs=rows[:], start=True, stop=True)
        keep_warm(1)
        vectors = keep.tile([P, PARTS + PERSP * PARTS], F32)
        weight_sq = keep.tile([P, PARTS, PERSP], F32)
        weight_bias = keep.tile([P, PARTS, PERSP], F32)
        half_bias = keep.tile([P, FEAT], F32)
        weight_columns = vectors[:, PARTS : PARTS + PERSP * PARTS].rearrange("f (p m) -> f m p", m=PARTS)
        nc.vector.tensor_copy(out=vectors[:], in_=vector_bank[:, 0 : PARTS + PERSP * PARTS])
        quantise_pair(hm_mx, 0)
        quantise_weight(1)
        nc.vector.tensor_tensor(out=weight_sq[:], in0=weight_columns, in1=weight_columns, op=ALU.mult)

        def bias_column(m):
            return vectors[:, m : m + 1]

        def weight_column(p, m):
            j = PARTS + PARTS * p + m
            return vectors[:, j : j + 1]

        adj_flipped = [flip_chunk(adj_sb, c, c - 2) for c in (2, 3)]
        group_chunk(adj_mx, 2, adj_flipped[0], scalar_copy)
        nc.scalar.activation(out=half_bias[:], in_=bias_bank[:], func=ACT.Copy, scale=0.5)
        nc.vector.tensor_tensor(
            out=weight_bias[:],
            in0=weight_columns,
            in1=vectors[:, 0:PARTS].unsqueeze(2).to_broadcast([P, PARTS, PERSP]),
            op=ALU.mult,
        )
        group_chunk(adj_mx, 3, adj_flipped[1], vector_copy)
        keep_warm(1)

        all_nodes = slice(0, NODES)
        pair_nodes = [slice(pair * HALF, (pair + 1) * HALF) for pair in range(PAIRS)]

        def multiply_z(tag, m, nodes):
            operand = (adj_mx, hm_mx)[m]
            bank = psum.tile([P, nodes.stop - nodes.start], F32, tag=tag, name="z")
            nc.tensor.matmul_mx(
                out=bank[:],
                lhsT=weight_codes[:, m, :].bitcast(FP8X4),
                lhsT_scale=weight_scales[:, m, :],
                rhs=operand["codes"][:, nodes].bitcast(FP8X4),
                rhs_scale=operand["scales"][:, nodes],
                start=True,
                stop=True,
            )
            return bank

        def keep_warm_mx(tag, nodes):
            multiply_z(tag, 0, nodes)

        squares = keep.tile([P, PARTS, NODES], F32)
        weighted = keep.tile([P, PERSP, PARTS, NODES], F32)
        norm_floor = keep.tile([P, CHUNKS, PERSP], F32)
        inv_norm = keep.tile([P, CHUNKS, PERSP], F32)

        def square(m, pair, z):
            nc.scalar.activation(
                out=squares[:, m, pair_nodes[pair]], in_=z[:], func=ACT.Square, bias=bias_column(m)
            )

        def weigh_on_scalar(p, m, pair, z):
            nc.scalar.activation(
                out=weighted[:, p, m, pair_nodes[pair]],
                in_=z[:],
                func=ACT.Identity,
                scale=weight_column(p, m),
                bias=weight_bias[:, m, p : p + 1],
            )

        def weigh_on_vector(p, m, pair, z):
            nc.vector.tensor_scalar(
                out=weighted[:, p, m, pair_nodes[pair]],
                in0=z[:],
                scalar1=bias_column(m),
                scalar2=weight_column(p, m),
                op0=ALU.add,
                op1=ALU.mult,
            )

        norm_banks = []

        def sum_squares(m, pair):
            if m == 0:
                norm_banks.append(psum.tile([P, 2, PERSP], F32, tag="bank%d" % pair, name="norm_bank"))
            for j in range(2):
                c = 2 * pair + j
                nc.tensor.matmul(
                    out=norm_banks[pair][:, j, :],
                    lhsT=squares[:, m, c * P : (c + 1) * P],
                    rhs=weight_sq[:, m, :],
                    start=(m == 0 and j == 0),
                    stop=(m == PARTS - 1 and j == 1),
                )

        def floor_norms(pair):
            nc.vector.tensor_scalar_max(
                out=norm_floor[:, 2 * pair : 2 * pair + 2, :], in0=norm_banks[pair][:], scalar1=EPS * EPS
            )

        def invert_norms(pair):
            chunks = slice(2 * pair, 2 * pair + 2)
            nc.scalar.activation(
                out=inv_norm[:, chunks, :], in_=norm_floor[:, chunks, :], func=ACT.Abs_reciprocal_sqrt
            )

        spread_banks = []

        def spread_norms(c, tag):
            bank = psum.tile([P, PERSP, P], F32, tag=tag, name="spread_bank")
            for p in range(PERSP):
                nc.tensor.transpose(bank[:, p, :], inv_norm[:, c, p : p + 1].to_broadcast([P, P]), ident_f32[:])
            spread_banks.append(bank)

        z1_first = multiply_z("bank4", 0, pair_nodes[0])
        square(0, 0, z1_first)
        hm_flipped = [flip_chunk(hm_sb, c, c) for c in (2, 3)]
        group_chunk(hm_mx, 2, hm_flipped[0], scalar_copy)
        group_chunk(hm_mx, 3, hm_flipped[1], vector_copy)
        z2_first = multiply_z("bank5", 1, pair_nodes[0])
        z2_vector = multiply_z("bank6", 1, pair_nodes[0])
        keep_warm_mx("bank7", pair_nodes[0])
        quantise_pair(adj_mx, 1)
        quantise_pair(hm_mx, 1)
        square(1, 0, z2_first)
        sum_squares(0, 0)
        z1_second = multiply_z("bank7", 0, pair_nodes[1])
        sum_squares(1, 0)
        for p in range(PERSP):
            weigh_on_scalar(p, 0, 0, z1_first)
        weigh_on_vector(0, 1, 0, z2_vector)
        floor_norms(0)
        weigh_on_vector(1, 1, 0, z2_vector)
        z2_second = multiply_z("bank2", 1, pair_nodes[1])
        square(0, 1, z1_second)
        invert_norms(0)
        keep_warm_mx("bank5", all_nodes)
        sum_squares(0, 1)
        spread_norms(0, "bank3")
        square(1, 1, z2_second)
        spread_norms(1, "bank6")
        sum_squares(1, 1)
        for p in range(PERSP):
            weigh_on_scalar(p, 0, 1, z1_second)
        for p in range(PERSP):
            weigh_on_scalar(p, 1, 1, z2_second)

        sum_bank = psum.tile([P, CHUNKS, FEAT], F32, tag="bank4")

        def multiply_sum(c):
            nodes = slice(c * P, (c + 1) * P)
            for m, operand in enumerate((adj_mx, hm_mx)):
                nc.tensor.matmul_mx(
                    out=sum_bank[:, c, :],
                    lhsT=operand["codes"][:, nodes].bitcast(FP8X4),
                    lhsT_scale=operand["scales"][:, nodes],
                    rhs=weight_codes[:, m, :].bitcast(FP8X4),
                    rhs_scale=weight_scales[:, m, :],
                    start=(m == 0),
                    stop=(m == PARTS - 1),
                )

        for c in range(CHUNKS):
            multiply_sum(c)
        keep_warm_mx("bank3", all_nodes)

        half_adj = keep.tile([P, CHUNKS, NODES], BF16)

        def halve_adj(c):
            nc.scalar.mul(out=half_adj[:, c, :], in_=adj_sb[:, c, :], mul=0.5)

        cf_grouped = keep.tile([P, CHUNKS, P, PACK], BF16, align_bytes=64)
        cf_codes = keep.tile([P, NODES], U32, align_bytes=64)
        cf_scales = keep.tile([P, NODES], U8, align_bytes=64)

        def normalise(c):
            nc.vector.tensor_tensor(
                out=cf_grouped[:, c].rearrange("q n (p m) -> q n p m", m=PARTS),
                in0=weighted[:, :, :, c * P : (c + 1) * P].rearrange("q p m n -> q n p m"),
                in1=spread_banks[c][:].rearrange("q p n -> q n p").unsqueeze(3).to_broadcast([P, P, PERSP, PARTS]),
                op=ALU.mult,
            )

        def quantise_cf(c):
            nodes = slice(c * P, (c + 1) * P)
            nc.vector.quantize_mx(
                out=cf_codes[:, nodes].bitcast(FP8X4),
                scales=cf_scales[:, nodes],
                in_=cf_grouped[:, c].rearrange("q n t -> q (n t)"),
            )

        def multiply_cf(out, c, columns):
            nodes = slice(c * P, (c + 1) * P)
            nc.tensor.matmul_mx(
                out=out,
                lhsT=cf_codes[:, nodes].bitcast(FP8X4),
                lhsT_scale=cf_scales[:, nodes],
                rhs=cf_codes[:, columns].bitcast(FP8X4),
                rhs_scale=cf_scales[:, columns],
                start=True,
                stop=True,
            )

        masked = keep.tile([P, CHUNKS, NODES], F32)
        half_sum = keep.tile([P, PAIRS, 2], F32)
        first_twice = keep.tile([P, 2], F32)
        row_sum = keep.tile([P, CHUNKS], F32)
        twice_sum = keep.tile([P, CHUNKS], F32)
        half_inv_sum = keep.tile([P, CHUNKS], F32)
        quarter_inv_sum = keep.tile([P, 2], F32)
        adj = keep.tile([P, CHUNKS, NODES], F32)
        adj_rows = out_1.rearrange("(h q j) m -> h q j m", h=PAIRS, j=2)

        def mask_half(c, pair):
            nc.scalar.activation(
                out=masked[:, c, pair_nodes[pair]].rearrange("n (q j) -> n q j", j=2),
                in_=att_halves[pair][c][:].rearrange("n (j q) -> n q j", j=2),
                func=ACT.Relu,
                scale=1.0 + pair,
                accum_out=half_sum[:, pair, c : c + 1],
            )

        def mask_and_sum(c):
            nc.scalar.activation(
                out=masked[:, c, :].rearrange("n (h q j) -> n h q j", h=PAIRS, j=2),
                in_=att_rows[c][:].rearrange("n (h j q) -> n h q j", h=PAIRS, j=2),
                func=ACT.Relu,
                accum_out=row_sum[:, c : c + 1],
            )

        normalise(0)
        floor_norms(1)
        invert_norms(1)
        for c in range(CHUNKS):
            halve_adj(c)
        for c, tag in ((2, "bank5"), (3, "bank0")):
            spread_norms(c, tag)
        normalise(1)
        quantise_cf(0)
        quantise_cf(1)
        for tag in ("bank6", "bank1"):
            keep_warm_mx(tag, all_nodes)
        att_halves = [
            [psum.tile([P, HALF], F32, tag=tag, name="att_half") for tag in tags]
            for tags in (("bank7", "bank2"), ("bank0", "bank6"))
        ]
        for c in (0, 1):
            multiply_cf(att_halves[0][c][:], c, pair_nodes[0])
            mask_half(c, 0)
        normalise(2)
        normalise(3)
        quantise_cf(2)
        quantise_cf(3)
        for tag in ("bank3", "bank5"):
            keep_warm_mx(tag, all_nodes)
        att_rows = {c: psum.tile([P, NODES], F32, tag=tag, name="att_row") for c, tag in ((2, "bank1"), (3, "bank3"))}
        for c in (0, 1):
            multiply_cf(att_halves[1][c][:], c, pair_nodes[1])
        for c in (2, 3):
            multiply_cf(att_rows[c][:], c, all_nodes)
        for c in (0, 1):
            mask_half(c, 1)
        for c in (2, 3):
            mask_and_sum(c)

        output = keep.tile([P, CHUNKS, FEAT], F32)
        nc.vector.scalar_tensor_tensor(
            out=output[:],
            in0=sum_bank[:],
            scalar=0.5,
            in1=half_bias[:].unsqueeze(1).to_broadcast([P, CHUNKS, FEAT]),
            op0=ALU.mult,
            op1=ALU.add,
        )
        nc.sync.dma_start(
            out=out_0.rearrange("(h q j) f -> q h j f", h=PAIRS, j=2),
            in_=output[:].rearrange("q (h j) f -> q h j f", h=PAIRS),
        )

        def floor_sum(c):
            nc.vector.tensor_scalar(
                out=twice_sum[:, c : c + 1],
                in0=row_sum[:, c : c + 1],
                scalar1=2 * EPS,
                scalar2=2.0,
                op0=ALU.max,
                op1=ALU.mult,
            )

        def invert_sum(c):
            nc.vector.reciprocal(out=half_inv_sum[:, c : c + 1], in_=twice_sum[:, c : c + 1])

        def average(c, columns, factor):
            nc.vector.scalar_tensor_tensor(
                out=adj[:, c, columns],
                in0=masked[:, c, columns],
                scalar=factor,
                in1=half_adj[:, c, columns],
                op0=ALU.mult,
                op1=ALU.add,
            )
            nc.sync.dma_start(out=adj_rows[c // 2][:, c % 2, columns], in_=adj[:, c, columns])

        def join_sums(c):
            nc.vector.tensor_scalar(
                out=twice_sum[:, c : c + 1],
                in0=half_sum[:, 1, c : c + 1],
                scalar1=first_twice[:, c : c + 1],
                scalar2=4 * EPS,
                op0=ALU.add,
                op1=ALU.max,
            )

        def halve_factor(c):
            nc.vector.tensor_scalar_mul(
                out=quarter_inv_sum[:, c : c + 1], in0=half_inv_sum[:, c : c + 1], scalar1=0.5
            )

        def average_half(c, pair):
            factor = quarter_inv_sum if (c < 2 and pair == 1) else half_inv_sum
            average(c, pair_nodes[pair], factor[:, c : c + 1])

        nc.vector.tensor_scalar_mul(out=first_twice[:], in0=half_sum[:, 0, :], scalar1=2.0)
        join_sums(0)
        invert_sum(0)
        join_sums(1)
        halve_factor(0)
        average_half(0, 0)
        invert_sum(1)
        average_half(0, 1)
        halve_factor(1)
        floor_sum(2)
        average_half(1, 0)
        invert_sum(2)
        average_half(1, 1)
        floor_sum(3)
        average_half(2, 0)
        invert_sum(3)
        average_half(2, 1)
        average_half(3, 0)
        average_half(3, 1)
